import numpy as np
import ml_dtypes


def mxq(x, axis, fmt="e4m3"):
    dtype, down = {"e4m3": (ml_dtypes.float8_e4m3fn, 7), "e5m2": (ml_dtypes.float8_e5m2, 14)}[fmt]
    v = np.moveaxis(np.asarray(x, np.float32).astype(ml_dtypes.bfloat16).astype(np.float64), axis, -1)
    blocks = v.reshape(v.shape[:-1] + (-1, 32))
    amax = np.abs(blocks).max(-1, keepdims=True)
    byte = np.maximum(np.where(amax > 0, np.frexp(amax)[1] - 1 + 127, 0) - down, 1)
    scale = np.exp2(byte - 127.0)
    codes = (blocks / scale).astype(np.float32).astype(dtype).astype(np.float64)
    return np.moveaxis((codes * scale).reshape(v.shape), -1, axis)


WIDE = False


def mx_kscale(k):
    if not WIDE:
        return np.ones(k)
    levels = np.array([10, -10, 5, -5, 0])
    if k % 512:
        return np.exp2(np.random.permutation(np.resize(levels, k // 32))).repeat(32)
    a = np.empty((k // 512, 16))
    for p in range(k // 512):
        a[p, :8] = np.random.permutation(np.resize(levels, 8))
        for g in range(8):
            far = levels[np.abs(levels - a[p, g]) >= 10]
            a[p, g + 8] = far[np.random.randint(len(far))]
    return np.exp2(a.ravel()).repeat(32)


BF16 = ml_dtypes.bfloat16


def bf(x):
    return np.asarray(x, np.float32).astype(BF16)


def f64(x):
    return np.asarray(x).astype(np.float64)


B, S, D, O = 2, 256, 2048, 4096

EPS = 1.0 / 137.0


def setup_inputs():
    s = mx_kscale(D)
    p = np.exp2(np.round(0.5 * np.log2(np.mean(1.0 / (s * s)))))
    q = np.exp2(np.round(0.5 * np.log2(np.mean(s * s))))
    return {"x": bf(np.random.standard_normal((B, S, D)) * 0.5 * s * p),
            "kernel": bf(np.random.standard_normal((D, O)) * 0.5 / s[:, None] * q),
            "bias": bf(np.random.standard_normal(O) * 0.1),
            "alpha": bf(1.0 + 0.1 * np.random.standard_normal(1))}


def core(x, kernel, bias, alpha):
    xf, kf = f64(x), f64(kernel)
    y = mxq(xf, 2, "e4m3") @ mxq(kf, 0, "e4m3")
    x_sq = np.sum(xf * xf, axis=-1, keepdims=True)
    k_sq = np.sum(kf * kf, axis=0, keepdims=True)
    distances = x_sq + k_sq - 2.0 * y
    y = (y * y) / (distances + EPS)
    y = y + f64(bias).reshape((1,) * (y.ndim - 1) + (-1,))
    scale = (np.sqrt(float(O)) / np.log1p(float(O))) ** f64(alpha)
    return y * scale


def e4m3fn_bytes(y):
    return np.clip(np.asarray(y, np.float64), -448.0, 448.0).astype(np.float32).astype(ml_dtypes.float8_e4m3fn).view(np.uint8)


def reference(x, kernel, bias, alpha):
    out = core(x, kernel, bias, alpha)
    s = np.max(np.abs(out)) / 448.0
    return out, e4m3fn_bytes(out / s)

@@ -1,0 +1,332 @@
+import math
+from contextlib import ExitStack
+
+import concourse.mybir as mybir
+from concourse.masks import make_identity
+
+F32 = mybir.dt.float32
+BF16 = mybir.dt.bfloat16
+U32 = mybir.dt.uint32
+U8 = mybir.dt.uint8
+FP8X4 = mybir.dt.float8_e4m3fn_x4
+FP8 = mybir.dt.float8_e4m3fn
+ALU = mybir.AluOpType
+ACT = mybir.ActivationFunctionType
+AX = mybir.AxisListType
+
+P = 128
+TOK = 512
+D = 2048
+O = 4096
+NB = 8
+NW = 512
+NG = 4
+NM = 4
+NSTEP = NB * NM
+EPS = 1.0 / 137.0
+LOG_RATIO = math.log(math.sqrt(4096.0) / math.log(1.0 + 4096.0))
+S_UNITS = (9, 17, 25)
+CV = 1408
+
+FLOPS = 2 * TOK * D * O
+
+
+def tile_yatnmn_kernel(tc, x, kernel, bias, alpha, out_0, out_1):
+    nc = tc.nc
+    xf = x.flatten_outer_dims()
+    o0 = out_0.flatten_outer_dims()
+    o1 = out_1.flatten_outer_dims()
+
+    with ExitStack() as ctx:
+        keep = ctx.enter_context(tc.tile_pool(name="keep", bufs=1))
+        rawp = ctx.enter_context(tc.tile_pool(name="rawp", bufs=12))
+        grpp = ctx.enter_context(tc.tile_pool(name="grpp", bufs=4))
+        codp = ctx.enter_context(tc.tile_pool(name="codp", bufs=10))
+        tmpp = ctx.enter_context(tc.tile_pool(name="tmpp", bufs=4))
+        smlp = ctx.enter_context(tc.tile_pool(name="smlp", bufs=2))
+        psy = ctx.enter_context(tc.psum_pool(name="psy", bufs=4))
+        psk = ctx.enter_context(tc.psum_pool(name="psk", bufs=3))
+        psm = ctx.enter_context(tc.psum_pool(name="psm", bufs=1))
+
+        out_sb = keep.tile([P, NM, O], F32, name="out_sb")
+        q8 = keep.tile([P, NM, O], FP8, name="q8")
+        b_c = keep.tile([P, O], F32, name="b_c")
+        xc = keep.tile([P, NG, TOK], U32, name="xc", align_bytes=64)
+        xs = keep.tile([P, NG, TOK], U8, name="xs", align_bytes=64)
+        ident_bf = keep.tile([P, P], BF16, name="ident_bf")
+        ident_f = keep.tile([P, P], F32, name="ident_f")
+        alpha_t = keep.tile([P, 1], BF16, name="alpha_t")
+        c_t = keep.tile([P, 1], F32, name="c_t")
+        sc_t = keep.tile([P, 1], F32, name="sc_t")
+        dummy = keep.tile([P, 1], F32, name="dummy")
+        zero = keep.tile([P, 1], F32, name="zero")
+        xsq = keep.tile([P, NM], F32, name="xsq")
+        xsqe = keep.tile([P, NM], F32, name="xsqe")
+        ksq_cols = keep.tile([P, 2 * NSTEP], F32, name="ksq_cols")
+        amax_cols = keep.tile([P, NSTEP], F32, name="amax_cols")
+        pmax = keep.tile([P, 1], F32, name="pmax")
+        amax = keep.tile([P, 1], F32, name="amax")
+        ramax = keep.tile([P, 1], F32, name="ramax")
+        fac = keep.tile([P, 1], F32, name="fac")
+
+        raw = {}
+        grp = {}
+        kc = {}
+        ks = {}
+        kts = {}
+        k4s = {}
+        kbs = {}
+        ksbs = {}
+        ys = {}
+        t1s = {}
+        t2s = {}
+        xsb = {}
+        xts = {}
+        xgs = {}
+        stg = {}
+
+        def load_raw(q):
+            nb, g = divmod(q, NG)
+            t = rawp.tile([P, 4, NW], BF16, name="raw%d" % q, tag="raw")
+            nc.sync.dma_start(
+                out=t[:],
+                in_=kernel[512 * g:512 * (g + 1), NW * nb:NW * (nb + 1)].rearrange("(p j) w -> p j w", j=4),
+            )
+            raw[q] = t
+
+        def load_x(m):
+            t = rawp.tile([P, D], BF16, name="xsb%d" % m, tag="raw")
+            nc.sync.dma_start(out=t[:], in_=xf[P * m:P * (m + 1), :])
+            xsb[m] = t
+
+        def load_bias(h):
+            t = rawp.tile([P, D], BF16, name="stg%d" % h, tag="raw")
+            nc.sync.dma_start(out=t[:], in_=bias[D * h:D * (h + 1)].partition_broadcast(P))
+            stg[h] = t
+
+        def x_square(m):
+            junk = smlp.tile([P, D], BF16, name="junkx%d" % m, tag="junk")
+            nc.scalar.activation(out=junk[:], in_=xsb[m][:], func=ACT.Square, accum_out=xsq[:, m:m + 1])
+
+        def x_trans(g):
+            for mp in range(2):
+                xt = psk.tile([P, 2, 256], F32, name="xt%d_%d" % (g, mp), tag="kT")
+                for mi in range(2):
+                    words = xsb[2 * mp + mi][:].bitcast(F32)
+                    for u in range(2):
+                        nc.tensor.transpose(
+                            out=xt[:, u, P * mi:P * (mi + 1)],
+                            in_=words[:, 256 * g + u:256 * (g + 1):2],
+                            identity=ident_f[:],
+                        )
+                xts[(g, mp)] = xt
+
+        def x_evac(g):
+            xg = grpp.tile([P, TOK, 4], BF16, name="xg%d" % g, tag="grp", align_bytes=64)
+            for mp in range(2):
+                nc.vector.tensor_copy(
+                    out=xg[:, 256 * mp:256 * (mp + 1), :].bitcast(F32),
+                    in_=xts[(g, mp)][:].rearrange("p u r -> p r u"),
+                )
+            xgs[g] = xg
+
+        def x_quant(g):
+            nc.vector.quantize_mx(
+                out=xc[:, g, :].bitcast(FP8X4),
+                scales=xs[:, g, :],
+                in_=xgs[g][:].rearrange("p r j -> p (r j)"),
+            )
+
+        def inter_alloc(q):
+            grp[q] = grpp.tile([P, NW, 4], BF16, name="grp%d" % q, tag="grp", align_bytes=64)
+
+        def inter_v(q):
+            if q not in S_UNITS:
+                nc.vector.tensor_copy(out=grp[q][:], in_=raw[q][:].rearrange("p j w -> p w j"))
+
+        def inter_s(q):
+            if q in S_UNITS:
+                nc.scalar.copy(out=grp[q][:], in_=raw[q][:].rearrange("p j w -> p w j"))
+
+        def quant(q):
+            c = codp.tile([P, NW], U32, name="kc%d" % q, tag="kc", align_bytes=64)
+            s = codp.tile([P, NW], U8, name="ks%d" % q, tag="ks", align_bytes=64)
+            nc.vector.quantize_mx(out=c[:].bitcast(FP8X4), scales=s[:], in_=grp[q][:].rearrange("p w j -> p (w j)"))
+            kc[q] = c
+            ks[q] = s
+
+        def ktrans(t):
+            nb, r = divmod(t, 8)
+            h, ob = divmod(r, 4)
+            kt = psk.tile([P, 8 * P], BF16, name="kt%d" % t, tag="kT")
+            for i in range(8):
+                g = 2 * h + i // 4
+                j = i % 4
+                nc.tensor.transpose(
+                    out=kt[:, P * i:P * (i + 1)],
+                    in_=raw[NG * nb + g][:, j, P * ob:P * (ob + 1)],
+                    identity=ident_bf[:],
+                )
+            kts[t] = kt
+
+        def ksq_act(t):
+            nb, r = divmod(t, 8)
+            h, ob = divmod(r, 4)
+            col = 8 * nb + 2 * ob + h
+            junk = smlp.tile([P, 8 * P], BF16, name="junk%d" % t, tag="junk")
+            nc.scalar.activation(out=junk[:], in_=kts[t][:], func=ACT.Square, accum_out=ksq_cols[:, col:col + 1])
+
+        def ksq_reduce(nb):
+            k4 = smlp.tile([P, 4], F32, name="k4_%d" % nb, tag="k4")
+            nc.vector.tensor_reduce(
+                out=k4[:],
+                in_=ksq_cols[:, 8 * nb:8 * (nb + 1)].rearrange("p (o h) -> p o h", h=2),
+                axis=AX.X,
+                op=ALU.add,
+            )
+            k4s[nb] = k4
+
+        def ksq_bcast(nb):
+            kb = psm.tile([P, NW], F32, name="kb%d" % nb, tag="misc")
+            for ob in range(4):
+                nc.tensor.transpose(
+                    out=kb[:, P * ob:P * (ob + 1)],
+                    in_=k4s[nb][:, ob:ob + 1].to_broadcast([P, P]),
+                    identity=ident_f[:],
+                )
+            kbs[nb] = kb
+
+        def ksq_evac(nb):
+            ksb = smlp.tile([P, NW], F32, name="ksb%d" % nb, tag="ksb")
+            nc.scalar.copy(out=ksb[:], in_=kbs[nb][:])
+            ksbs[nb] = ksb
+
+        def mx(s):
+            nb, m = divmod(s, NM)
+            y = psy.tile([P, NW], F32, name="y%d" % s, tag="y")
+            for g in range(NG):
+                nc.tensor.matmul_mx(
+                    out=y[:],
+                    lhsT=xc[:, g, P * m:P * (m + 1)].bitcast(FP8X4),
+                    lhsT_scale=xs[:, g, P * m:P * (m + 1)],
+                    rhs=kc[NG * nb + g][:].bitcast(FP8X4),
+                    rhs_scale=ks[NG * nb + g][:],
+                    start=(g == 0),
+                    stop=(g == NG - 1),
+                )
+            ys[s] = y
+
+        def dprime(s):
+            nb, m = divmod(s, NM)
+            t1 = tmpp.tile([P, NW], F32, name="t1_%d" % s, tag="t1")
+            nc.vector.scalar_tensor_tensor(
+                out=t1[:], in0=ys[s][:], scalar=-2.0, in1=ksbs[nb][:], op0=ALU.mult, op1=ALU.add
+            )
+            t1s[s] = t1
+
+        def ars(s):
+            nb, m = divmod(s, NM)
+            nc.scalar.activation(
+                out=t1s[s][:], in_=t1s[s][:], func=ACT.Abs_reciprocal_sqrt, bias=xsqe[:, m:m + 1], scale=1.0
+            )
+
+        def umul(s):
+            t2 = tmpp.tile([P, NW], F32, name="t2_%d" % s, tag="t2")
+            nc.vector.tensor_tensor(out=t2[:], in0=ys[s][:], in1=t1s[s][:], op=ALU.mult)
+            t2s[s] = t2
+
+        def square(s):
+            nc.scalar.activation(out=t2s[s][:], in_=t2s[s][:], func=ACT.Square, scale=sc_t[:, 0:1])
+
+        def addb(s):
+            nb, m = divmod(s, NM)
+            cols = slice(NW * nb, NW * (nb + 1))
+            nc.vector.tensor_tensor(out=out_sb[:, m, cols], in0=t2s[s][:], in1=b_c[:, cols], op=ALU.add)
+            nc.vector.tensor_reduce(
+                out=amax_cols[:, s:s + 1], in_=out_sb[:, m, cols], axis=AX.X, op=ALU.max, apply_absolute_value=True
+            )
+            nc.sync.dma_start(out=o0[P * m:P * (m + 1), cols], in_=out_sb[:, m, cols])
+
+        nc.scalar.dma_start(out=alpha_t[:], in_=alpha.partition_broadcast(P))
+        load_raw(0)
+        for m in range(NM):
+            load_x(m)
+        for q in range(1, 6):
+            load_raw(q)
+        load_bias(0)
+        load_bias(1)
+
+        make_identity(nc, ident_f[:])
+        make_identity(nc, ident_bf[:])
+        nc.vector.memset(zero[:], 0.0)
+        nc.scalar.activation(out=c_t[:], in_=alpha_t[:], func=ACT.Exp, scale=LOG_RATIO)
+        nc.scalar.activation(out=sc_t[:], in_=alpha_t[:], func=ACT.Exp, scale=0.5 * LOG_RATIO)
+        nc.scalar.activation(out=dummy[:], in_=c_t[:], func=ACT.Abs_reciprocal_sqrt)
+
+        for tau in range(-6, NSTEP + 2):
+            tq = tau + 6
+            if 6 <= tau + 12 < NSTEP:
+                load_raw(tau + 12)
+            if tq < NG:
+                x_trans(tq)
+            if tq < NSTEP:
+                ktrans(2 * tq)
+                ktrans(2 * tq + 1)
+            if 0 <= tau + 1 < NSTEP:
+                mx(tau + 1)
+            if tq >= 5 and (tq - 5) % 4 == 0 and (tq - 5) // 4 < NB:
+                ksq_evac((tq - 5) // 4)
+            if tq < NSTEP:
+                ksq_act(2 * tq)
+            if 0 <= tau < NSTEP:
+                dprime(tau)
+                ars(tau)
+            if 0 <= tau - 1 < NSTEP:
+                umul(tau - 1)
+                square(tau - 1)
+            if tq >= 4 and (tq - 4) % 4 == 0 and (tq - 4) // 4 < NB:
+                ksq_reduce((tq - 4) // 4)
+                ksq_bcast((tq - 4) // 4)
+            if tq < NG:
+                x_evac(tq)
+                x_square(tq)
+            if tq < NSTEP:
+                inter_alloc(tq)
+                inter_v(tq)
+            if tq < NSTEP:
+                ksq_act(2 * tq + 1)
+                inter_s(tq)
+            if 0 <= tau - 2 < NSTEP:
+                addb(tau - 2)
+            if 1 <= tq <= NG:
+                x_quant(tq - 1)
+            if 1 <= tq <= NSTEP:
+                quant(tq - 1)
+            if tq == 3 or tq == 4:
+                h = tq - 3
+                nc.vector.tensor_scalar(
+                    out=b_c[:, D * h:D * (h + 1)], in0=stg[h][:], scalar1=c_t[:, 0:1], scalar2=None, op0=ALU.mult
+                )
+            if tq == 4:
+                nc.vector.tensor_scalar(out=xsqe[:], in0=xsq[:], scalar1=EPS, scalar2=None, op0=ALU.add)
+
+        nc.vector.tensor_reduce(out=pmax[:], in_=amax_cols[:], axis=AX.X, op=ALU.max)
+        pt = psm.tile([P, P], F32, name="pt", tag="misc")
+        nc.tensor.transpose(out=pt[:], in_=pmax[:, 0:1].to_broadcast([P, P]), identity=ident_f[:])
+        nc.vector.tensor_reduce(out=amax[:], in_=pt[:], axis=AX.X, op=ALU.max)
+        nc.vector.reciprocal(out=ramax[:], in_=amax[:])
+        nc.vector.tensor_scalar(out=fac[:], in0=ramax[:], scalar1=448.0, scalar2=None, op0=ALU.mult)
+        for m in range(NM):
+            for h in range(2):
+                c0 = 2048 * h
+                nc.vector.tensor_scalar(
+                    out=q8[:, m, c0:c0 + CV], in0=out_sb[:, m, c0:c0 + CV], scalar1=fac[:, 0:1], scalar2=None,
+                    op0=ALU.mult, saturate=False,
+                )
+                nc.scalar.activation(
+                    out=q8[:, m, c0 + CV:c0 + 2048], in_=out_sb[:, m, c0 + CV:c0 + 2048], func=ACT.Identity,
+                    scale=fac[:, 0:1], bias=zero[:, 0:1], saturate=False,
+                )
+                nc.sync.dma_start(
+                    out=o1[P * m:P * (m + 1), c0:c0 + 2048], in_=q8[:, m, c0:c0 + 2048].bitcast(U8)
+                )

@@ -25,7 +25,7 @@ NM = 4
 NSTEP = NB * NM
 EPS = 1.0 / 137.0
 LOG_RATIO = math.log(math.sqrt(4096.0) / math.log(1.0 + 4096.0))
-S_UNITS = (9, 17, 25)
+S_UNITS = (6, 12, 18, 24, 29)
 CV = 1408
 
 FLOPS = 2 * TOK * D * O
@@ -63,7 +63,7 @@ def tile_yatnmn_kernel(tc, x, kernel, bias, alpha, out_0, out_1):
         xsq = keep.tile([P, NM], F32, name="xsq")
         xsqe = keep.tile([P, NM], F32, name="xsqe")
         ksq_cols = keep.tile([P, 2 * NSTEP], F32, name="ksq_cols")
-        amax_cols = keep.tile([P, NSTEP], F32, name="amax_cols")
+        amax_cols = keep.tile([P, NSTEP // 2], F32, name="amax_cols")
         pmax = keep.tile([P, 1], F32, name="pmax")
         amax = keep.tile([P, 1], F32, name="amax")
         ramax = keep.tile([P, 1], F32, name="ramax")
@@ -84,6 +84,7 @@ def tile_yatnmn_kernel(tc, x, kernel, bias, alpha, out_0, out_1):
         xts = {}
         xgs = {}
         stg = {}
+        gxs = {}
 
         def load_raw(q):
             nb, g = divmod(q, NG)
@@ -104,9 +105,24 @@ def tile_yatnmn_kernel(tc, x, kernel, bias, alpha, out_0, out_1):
             nc.sync.dma_start(out=t[:], in_=bias[D * h:D * (h + 1)].partition_broadcast(P))
             stg[h] = t
 
-        def x_square(m):
-            junk = smlp.tile([P, D], BF16, name="junkx%d" % m, tag="junk")
-            nc.scalar.activation(out=junk[:], in_=xsb[m][:], func=ACT.Square, accum_out=xsq[:, m:m + 1])
+        def x_gram(g):
+            for m in range(NM):
+                if g == 0:
+                    gxs[m] = psy.tile([P, NW], F32, name="gx%d" % m, tag="y")
+                for j in range(4):
+                    xt_mj = xgs[g][:, P * m:P * (m + 1), j]
+                    nc.tensor.matmul(
+                        out=gxs[m][:, 0:P], lhsT=xt_mj, rhs=xt_mj,
+                        start=(g == 0 and j == 0), stop=(g == NG - 1 and j == 3),
+                    )
+
+        def x_diag():
+            for m in range(NM):
+                junkf = tmpp.tile([P, P], F32, name="junkf%d" % m, tag="t1")
+                nc.vector.scalar_tensor_tensor(
+                    out=junkf[:], in0=gxs[m][:, 0:P], scalar=1.0, in1=ident_f[:], op0=ALU.mult, op1=ALU.mult,
+                    accum_out=xsq[:, m:m + 1],
+                )
 
         def x_trans(g):
             for mp in range(2):
@@ -242,10 +258,16 @@ def tile_yatnmn_kernel(tc, x, kernel, bias, alpha, out_0, out_1):
             nb, m = divmod(s, NM)
             cols = slice(NW * nb, NW * (nb + 1))
             nc.vector.tensor_tensor(out=out_sb[:, m, cols], in0=t2s[s][:], in1=b_c[:, cols], op=ALU.add)
-            nc.vector.tensor_reduce(
-                out=amax_cols[:, s:s + 1], in_=out_sb[:, m, cols], axis=AX.X, op=ALU.max, apply_absolute_value=True
-            )
             nc.sync.dma_start(out=o0[P * m:P * (m + 1), cols], in_=out_sb[:, m, cols])
+
+        def absmax(s):
+            nb, m = divmod(s, NM)
+            if nb % 2 == 1:
+                k = nb // 2
+                nc.vector.tensor_reduce(
+                    out=amax_cols[:, NM * k + m:NM * k + m + 1], in_=out_sb[:, m, 2 * NW * k:2 * NW * (k + 1)],
+                    axis=AX.X, op=ALU.max, apply_absolute_value=True,
+                )
 
         nc.scalar.dma_start(out=alpha_t[:], in_=alpha.partition_broadcast(P))
         load_raw(0)
@@ -263,17 +285,19 @@ def tile_yatnmn_kernel(tc, x, kernel, bias, alpha, out_0, out_1):
         nc.scalar.activation(out=sc_t[:], in_=alpha_t[:], func=ACT.Exp, scale=0.5 * LOG_RATIO)
         nc.scalar.activation(out=dummy[:], in_=c_t[:], func=ACT.Abs_reciprocal_sqrt)
 
-        for tau in range(-6, NSTEP + 2):
+        for tau in range(-6, NSTEP + 3):
             tq = tau + 6
             if 6 <= tau + 12 < NSTEP:
                 load_raw(tau + 12)
+            if 0 <= tau + 1 < NSTEP:
+                mx(tau + 1)
             if tq < NG:
                 x_trans(tq)
+            if 1 <= tq <= NG:
+                x_gram(tq - 1)
             if tq < NSTEP:
                 ktrans(2 * tq)
                 ktrans(2 * tq + 1)
-            if 0 <= tau + 1 < NSTEP:
-                mx(tau + 1)
             if tq >= 5 and (tq - 5) % 4 == 0 and (tq - 5) // 4 < NB:
                 ksq_evac((tq - 5) // 4)
             if tq < NSTEP:
@@ -289,7 +313,6 @@ def tile_yatnmn_kernel(tc, x, kernel, bias, alpha, out_0, out_1):
                 ksq_bcast((tq - 4) // 4)
             if tq < NG:
                 x_evac(tq)
-                x_square(tq)
             if tq < NSTEP:
                 inter_alloc(tq)
                 inter_v(tq)
@@ -302,12 +325,15 @@ def tile_yatnmn_kernel(tc, x, kernel, bias, alpha, out_0, out_1):
                 x_quant(tq - 1)
             if 1 <= tq <= NSTEP:
                 quant(tq - 1)
+            if 0 <= tau - 3 < NSTEP:
+                absmax(tau - 3)
             if tq == 3 or tq == 4:
                 h = tq - 3
                 nc.vector.tensor_scalar(
                     out=b_c[:, D * h:D * (h + 1)], in0=stg[h][:], scalar1=c_t[:, 0:1], scalar2=None, op0=ALU.mult
                 )
             if tq == 4:
+                x_diag()
                 nc.vector.tensor_scalar(out=xsqe[:], in0=xsq[:], scalar1=EPS, scalar2=None, op0=ALU.add)
 
         nc.vector.tensor_reduce(out=pmax[:], in_=amax_cols[:], axis=AX.X, op=ALU.max)

@@ -25,7 +25,6 @@ NM = 4
 NSTEP = NB * NM
 EPS = 1.0 / 137.0
 LOG_RATIO = math.log(math.sqrt(4096.0) / math.log(1.0 + 4096.0))
-S_UNITS = (6, 12, 18, 24, 29)
 CV = 1408
 
 FLOPS = 2 * TOK * D * O
@@ -40,7 +39,7 @@ def tile_yatnmn_kernel(tc, x, kernel, bias, alpha, out_0, out_1):
     with ExitStack() as ctx:
         keep = ctx.enter_context(tc.tile_pool(name="keep", bufs=1))
         rawp = ctx.enter_context(tc.tile_pool(name="rawp", bufs=12))
-        grpp = ctx.enter_context(tc.tile_pool(name="grpp", bufs=4))
+        grpp = ctx.enter_context(tc.tile_pool(name="grpp", bufs=3))
         codp = ctx.enter_context(tc.tile_pool(name="codp", bufs=10))
         tmpp = ctx.enter_context(tc.tile_pool(name="tmpp", bufs=4))
         smlp = ctx.enter_context(tc.tile_pool(name="smlp", bufs=2))
@@ -63,7 +62,7 @@ def tile_yatnmn_kernel(tc, x, kernel, bias, alpha, out_0, out_1):
         xsq = keep.tile([P, NM], F32, name="xsq")
         xsqe = keep.tile([P, NM], F32, name="xsqe")
         ksq_cols = keep.tile([P, 2 * NSTEP], F32, name="ksq_cols")
-        amax_cols = keep.tile([P, NSTEP // 2], F32, name="amax_cols")
+        amax_cols = keep.tile([P, NSTEP], F32, name="amax_cols")
         pmax = keep.tile([P, 1], F32, name="pmax")
         amax = keep.tile([P, 1], F32, name="amax")
         ramax = keep.tile([P, 1], F32, name="ramax")
@@ -138,7 +137,7 @@ def tile_yatnmn_kernel(tc, x, kernel, bias, alpha, out_0, out_1):
                 xts[(g, mp)] = xt
 
         def x_evac(g):
-            xg = grpp.tile([P, TOK, 4], BF16, name="xg%d" % g, tag="grp", align_bytes=64)
+            xg = grpp.tile([P, TOK, 4], BF16, name="xg%d" % g, tag="xg", bufs=2, align_bytes=64)
             for mp in range(2):
                 nc.vector.tensor_copy(
                     out=xg[:, 256 * mp:256 * (mp + 1), :].bitcast(F32),
@@ -153,16 +152,16 @@ def tile_yatnmn_kernel(tc, x, kernel, bias, alpha, out_0, out_1):
                 in_=xgs[g][:].rearrange("p r j -> p (r j)"),
             )
 
-        def inter_alloc(q):
-            grp[q] = grpp.tile([P, NW, 4], BF16, name="grp%d" % q, tag="grp", align_bytes=64)
-
         def inter_v(q):
-            if q not in S_UNITS:
-                nc.vector.tensor_copy(out=grp[q][:], in_=raw[q][:].rearrange("p j w -> p w j"))
+            grp[q] = grpp.tile([P, NW, 4], BF16, name="grp%d" % q, tag="grpv", bufs=3, align_bytes=64)
+            nc.vector.tensor_copy(out=grp[q][:], in_=raw[q][:].rearrange("p j w -> p w j"))
 
-        def inter_s(q):
-            if q in S_UNITS:
-                nc.scalar.copy(out=grp[q][:], in_=raw[q][:].rearrange("p j w -> p w j"))
+        def inter_g(q):
+            grp[q] = grpp.tile([P, NW, 4], BF16, name="grp%d" % q, tag="grpg", bufs=1, align_bytes=64)
+            nc.gpsimd.tensor_scalar(
+                out=grp[q][:], in0=raw[q][:].rearrange("p j w -> p w j"), scalar1=1.0, scalar2=0.0,
+                op0=ALU.mult, op1=ALU.add,
+            )
 
         def quant(q):
             c = codp.tile([P, NW], U32, name="kc%d" % q, tag="kc", align_bytes=64)
@@ -262,18 +261,17 @@ def tile_yatnmn_kernel(tc, x, kernel, bias, alpha, out_0, out_1):
 
         def absmax(s):
             nb, m = divmod(s, NM)
-            if nb % 2 == 1:
-                k = nb // 2
-                nc.vector.tensor_reduce(
-                    out=amax_cols[:, NM * k + m:NM * k + m + 1], in_=out_sb[:, m, 2 * NW * k:2 * NW * (k + 1)],
-                    axis=AX.X, op=ALU.max, apply_absolute_value=True,
-                )
+            nc.vector.tensor_reduce(
+                out=amax_cols[:, s:s + 1], in_=out_sb[:, m, NW * nb:NW * (nb + 1)],
+                axis=AX.X, op=ALU.max, apply_absolute_value=True,
+            )
 
         nc.scalar.dma_start(out=alpha_t[:], in_=alpha.partition_broadcast(P))
         load_raw(0)
+        load_raw(1)
         for m in range(NM):
             load_x(m)
-        for q in range(1, 6):
+        for q in range(2, 6):
             load_raw(q)
         load_bias(0)
         load_bias(1)
@@ -285,56 +283,94 @@ def tile_yatnmn_kernel(tc, x, kernel, bias, alpha, out_0, out_1):
         nc.scalar.activation(out=sc_t[:], in_=alpha_t[:], func=ACT.Exp, scale=0.5 * LOG_RATIO)
         nc.scalar.activation(out=dummy[:], in_=c_t[:], func=ACT.Abs_reciprocal_sqrt)
 
-        for tau in range(-6, NSTEP + 3):
-            tq = tau + 6
-            if 6 <= tau + 12 < NSTEP:
-                load_raw(tau + 12)
-            if 0 <= tau + 1 < NSTEP:
-                mx(tau + 1)
-            if tq < NG:
-                x_trans(tq)
-            if 1 <= tq <= NG:
-                x_gram(tq - 1)
-            if tq < NSTEP:
-                ktrans(2 * tq)
-                ktrans(2 * tq + 1)
-            if tq >= 5 and (tq - 5) % 4 == 0 and (tq - 5) // 4 < NB:
-                ksq_evac((tq - 5) // 4)
-            if tq < NSTEP:
-                ksq_act(2 * tq)
-            if 0 <= tau < NSTEP:
-                dprime(tau)
-                ars(tau)
-            if 0 <= tau - 1 < NSTEP:
-                umul(tau - 1)
-                square(tau - 1)
-            if tq >= 4 and (tq - 4) % 4 == 0 and (tq - 4) // 4 < NB:
-                ksq_reduce((tq - 4) // 4)
-                ksq_bcast((tq - 4) // 4)
-            if tq < NG:
-                x_evac(tq)
-            if tq < NSTEP:
-                inter_alloc(tq)
-                inter_v(tq)
-            if tq < NSTEP:
-                ksq_act(2 * tq + 1)
-                inter_s(tq)
-            if 0 <= tau - 2 < NSTEP:
-                addb(tau - 2)
-            if 1 <= tq <= NG:
-                x_quant(tq - 1)
-            if 1 <= tq <= NSTEP:
-                quant(tq - 1)
-            if 0 <= tau - 3 < NSTEP:
-                absmax(tau - 3)
-            if tq == 3 or tq == 4:
-                h = tq - 3
-                nc.vector.tensor_scalar(
-                    out=b_c[:, D * h:D * (h + 1)], in0=stg[h][:], scalar1=c_t[:, 0:1], scalar2=None, op0=ALU.mult
-                )
-            if tq == 4:
-                x_diag()
-                nc.vector.tensor_scalar(out=xsqe[:], in0=xsq[:], scalar1=EPS, scalar2=None, op0=ALU.add)
+        def ok(s):
+            return 0 <= s < NSTEP
+
+        def okt(t):
+            return 0 <= t < 2 * NSTEP
+
+        def scale_bias(h):
+            nc.vector.tensor_scalar(
+                out=b_c[:, D * h:D * (h + 1)], in0=stg[h][:], scalar1=c_t[:, 0:1], scalar2=None, op0=ALU.mult
+            )
+
+        with tc.manual_schedule():
+            for k in range(-4, 18):
+                t0 = 4 * k + 12
+                due = (k + 1) % 2 == 0 and 0 <= (k + 1) // 2 < NB
+                nbd = (k + 1) // 2
+                for q in (2 * k + 12, 2 * k + 13):
+                    if 6 <= q < NSTEP:
+                        load_raw(q)
+                if ok(2 * k + 1):
+                    mx(2 * k + 1)
+                if due:
+                    ksq_reduce(nbd)
+                    ksq_bcast(nbd)
+                if ok(2 * k - 2):
+                    square(2 * k - 2)
+                if okt(t0 + 3):
+                    ktrans(t0 + 3)
+                for t in (t0, t0 + 1, t0 + 2):
+                    if okt(t):
+                        ksq_act(t)
+                if ok(2 * k + 8):
+                    inter_v(2 * k + 8)
+                if ok(2 * k - 3):
+                    addb(2 * k - 3)
+                if k == -3 or k == -2:
+                    x_quant(2 * k + 6)
+                if k == -1:
+                    scale_bias(0)
+                if ok(2 * k + 6):
+                    quant(2 * k + 6)
+                if ok(2 * k - 2):
+                    addb(2 * k - 2)
+                if k == -3 or k == -2:
+                    x_quant(2 * k + 7)
+                if k == -1:
+                    scale_bias(1)
+                if ok(2 * k + 7):
+                    quant(2 * k + 7)
+                if ok(2 * k + 9):
+                    inter_g(2 * k + 9)
+                if ok(2 * k + 2):
+                    mx(2 * k + 2)
+                for t in (t0 + 4, t0 + 5):
+                    if okt(t):
+                        ktrans(t)
+                if due:
+                    ksq_evac(nbd)
+                if ok(2 * k):
+                    dprime(2 * k)
+                    ars(2 * k)
+                if ok(2 * k - 1):
+                    umul(2 * k - 1)
+                    square(2 * k - 1)
+                if ok(2 * k - 3):
+                    absmax(2 * k - 3)
+                if okt(t0 + 3):
+                    ksq_act(t0 + 3)
+                if ok(2 * k + 1):
+                    dprime(2 * k + 1)
+                    ars(2 * k + 1)
+                if ok(2 * k - 2):
+                    absmax(2 * k - 2)
+                if ok(2 * k):
+                    umul(2 * k)
+                if okt(t0 + 6):
+                    ktrans(t0 + 6)
+                if k == -4 or k == -3:
+                    ga = 2 * k + 8
+                    x_trans(ga)
+                    x_trans(ga + 1)
+                    x_evac(ga)
+                    x_evac(ga + 1)
+                    x_gram(ga)
+                    x_gram(ga + 1)
+                if k == -2:
+                    x_diag()
+                    nc.vector.tensor_scalar(out=xsqe[:], in0=xsq[:], scalar1=EPS, scalar2=None, op0=ALU.add)
 
         nc.vector.tensor_reduce(out=pmax[:], in_=amax_cols[:], axis=AX.X, op=ALU.max)
         pt = psm.tile([P, P], F32, name="pt", tag="misc")

@@ -25,6 +25,8 @@ NM = 4
 NSTEP = NB * NM
 EPS = 1.0 / 137.0
 LOG_RATIO = math.log(math.sqrt(4096.0) / math.log(1.0 + 4096.0))
+G_ADD_FIRST = 23
+G_ADD_LAST = 29
 CV = 1408
 
 FLOPS = 2 * TOK * D * O
@@ -154,7 +156,10 @@ def tile_yatnmn_kernel(tc, x, kernel, bias, alpha, out_0, out_1):
 
         def inter_v(q):
             grp[q] = grpp.tile([P, NW, 4], BF16, name="grp%d" % q, tag="grpv", bufs=3, align_bytes=64)
-            nc.vector.tensor_copy(out=grp[q][:], in_=raw[q][:].rearrange("p j w -> p w j"))
+            nc.vector.tensor_copy(
+                out=grp[q][:].rearrange("p (c i) j -> p c j i", i=4),
+                in_=raw[q][:].rearrange("p j (c i) -> p c j i", i=4),
+            )
 
         def inter_g(q):
             grp[q] = grpp.tile([P, NW, 4], BF16, name="grp%d" % q, tag="grpg", bufs=1, align_bytes=64)
@@ -256,7 +261,10 @@ def tile_yatnmn_kernel(tc, x, kernel, bias, alpha, out_0, out_1):
         def addb(s):
             nb, m = divmod(s, NM)
             cols = slice(NW * nb, NW * (nb + 1))
-            nc.vector.tensor_tensor(out=out_sb[:, m, cols], in0=t2s[s][:], in1=b_c[:, cols], op=ALU.add)
+            if G_ADD_FIRST <= s <= G_ADD_LAST:
+                nc.gpsimd.tensor_tensor(out=out_sb[:, m, cols], in0=t2s[s][:], in1=b_c[:, cols], op=ALU.add)
+            else:
+                nc.vector.tensor_tensor(out=out_sb[:, m, cols], in0=t2s[s][:], in1=b_c[:, cols], op=ALU.add)
             nc.sync.dma_start(out=o0[P * m:P * (m + 1), cols], in_=out_sb[:, m, cols])
 
         def absmax(s):
@@ -290,9 +298,7 @@ def tile_yatnmn_kernel(tc, x, kernel, bias, alpha, out_0, out_1):
             return 0 <= t < 2 * NSTEP
 
         def scale_bias(h):
-            nc.vector.tensor_scalar(
-                out=b_c[:, D * h:D * (h + 1)], in0=stg[h][:], scalar1=c_t[:, 0:1], scalar2=None, op0=ALU.mult
-            )
+            nc.scalar.activation(out=b_c[:, D * h:D * (h + 1)], in_=stg[h][:], func=ACT.Copy, scale=c_t[:, 0:1])
 
         with tc.manual_schedule():
             for k in range(-4, 18):
@@ -304,6 +310,8 @@ def tile_yatnmn_kernel(tc, x, kernel, bias, alpha, out_0, out_1):
                         load_raw(q)
                 if ok(2 * k + 1):
                     mx(2 * k + 1)
+                if ok(2 * k + 2):
+                    mx(2 * k + 2)
                 if due:
                     ksq_reduce(nbd)
                     ksq_bcast(nbd)
@@ -320,22 +328,16 @@ def tile_yatnmn_kernel(tc, x, kernel, bias, alpha, out_0, out_1):
                     addb(2 * k - 3)
                 if k == -3 or k == -2:
                     x_quant(2 * k + 6)
-                if k == -1:
-                    scale_bias(0)
                 if ok(2 * k + 6):
                     quant(2 * k + 6)
                 if ok(2 * k - 2):
                     addb(2 * k - 2)
                 if k == -3 or k == -2:
                     x_quant(2 * k + 7)
-                if k == -1:
-                    scale_bias(1)
                 if ok(2 * k + 7):
                     quant(2 * k + 7)
                 if ok(2 * k + 9):
                     inter_g(2 * k + 9)
-                if ok(2 * k + 2):
-                    mx(2 * k + 2)
                 for t in (t0 + 4, t0 + 5):
                     if okt(t):
                         ktrans(t)
@@ -351,6 +353,9 @@ def tile_yatnmn_kernel(tc, x, kernel, bias, alpha, out_0, out_1):
                     absmax(2 * k - 3)
                 if okt(t0 + 3):
                     ksq_act(t0 + 3)
+                if k == -1:
+                    scale_bias(0)
+                    scale_bias(1)
                 if ok(2 * k + 1):
                     dprime(2 * k + 1)
                     ars(2 * k + 1)

@@ -25,8 +25,6 @@ NM = 4
 NSTEP = NB * NM
 EPS = 1.0 / 137.0
 LOG_RATIO = math.log(math.sqrt(4096.0) / math.log(1.0 + 4096.0))
-G_ADD_FIRST = 23
-G_ADD_LAST = 29
 CV = 1408
 
 FLOPS = 2 * TOK * D * O
@@ -40,7 +38,7 @@ def tile_yatnmn_kernel(tc, x, kernel, bias, alpha, out_0, out_1):
 
     with ExitStack() as ctx:
         keep = ctx.enter_context(tc.tile_pool(name="keep", bufs=1))
-        rawp = ctx.enter_context(tc.tile_pool(name="rawp", bufs=12))
+        rawp = ctx.enter_context(tc.tile_pool(name="rawp", bufs=11))
         grpp = ctx.enter_context(tc.tile_pool(name="grpp", bufs=3))
         codp = ctx.enter_context(tc.tile_pool(name="codp", bufs=10))
         tmpp = ctx.enter_context(tc.tile_pool(name="tmpp", bufs=4))
@@ -106,14 +104,31 @@ def tile_yatnmn_kernel(tc, x, kernel, bias, alpha, out_0, out_1):
             nc.sync.dma_start(out=t[:], in_=bias[D * h:D * (h + 1)].partition_broadcast(P))
             stg[h] = t
 
-        def x_gram(g):
-            for m in range(NM):
-                if g == 0:
-                    gxs[m] = psy.tile([P, NW], F32, name="gx%d" % m, tag="y")
+        def x_trans(m):
+            words = xsb[m][:].bitcast(F32)
+            for gp in range(2):
+                xt = psy.tile([P, 2, 2, P], F32, name="xt%d_%d" % (m, gp), tag="y")
+                for gi in range(2):
+                    g = 2 * gp + gi
+                    for u in range(2):
+                        nc.tensor.transpose(
+                            out=xt[:, gi, u, :], in_=words[:, 256 * g + u:256 * (g + 1):2], identity=ident_f[:]
+                        )
+                xts[(m, gp)] = xt
+
+        def x_evac(m):
+            for gp in range(2):
+                nc.vector.tensor_copy(
+                    out=xg[:, 2 * gp:2 * gp + 2, P * m:P * (m + 1), :].bitcast(F32),
+                    in_=xts[(m, gp)][:].rearrange("p g u r -> p g r u"),
+                )
+
+        def x_gram(m):
+            for g in range(NG):
                 for j in range(4):
-                    xt_mj = xgs[g][:, P * m:P * (m + 1), j]
+                    xt_mj = xg[:, g, P * m:P * (m + 1), j]
                     nc.tensor.matmul(
-                        out=gxs[m][:, 0:P], lhsT=xt_mj, rhs=xt_mj,
+                        out=gx[:, P * m:P * (m + 1)], lhsT=xt_mj, rhs=xt_mj,
                         start=(g == 0 and j == 0), stop=(g == NG - 1 and j == 3),
                     )
 
@@ -121,45 +136,27 @@ def tile_yatnmn_kernel(tc, x, kernel, bias, alpha, out_0, out_1):
             for m in range(NM):
                 junkf = tmpp.tile([P, P], F32, name="junkf%d" % m, tag="t1")
                 nc.vector.scalar_tensor_tensor(
-                    out=junkf[:], in0=gxs[m][:, 0:P], scalar=1.0, in1=ident_f[:], op0=ALU.mult, op1=ALU.mult,
-                    accum_out=xsq[:, m:m + 1],
+                    out=junkf[:], in0=gx[:, P * m:P * (m + 1)], scalar=1.0, in1=ident_f[:], op0=ALU.mult,
+                    op1=ALU.mult, accum_out=xsq[:, m:m + 1],
                 )
-
-        def x_trans(g):
-            for mp in range(2):
-                xt = psk.tile([P, 2, 256], F32, name="xt%d_%d" % (g, mp), tag="kT")
-                for mi in range(2):
-                    words = xsb[2 * mp + mi][:].bitcast(F32)
-                    for u in range(2):
-                        nc.tensor.transpose(
-                            out=xt[:, u, P * mi:P * (mi + 1)],
-                            in_=words[:, 256 * g + u:256 * (g + 1):2],
-                            identity=ident_f[:],
-                        )
-                xts[(g, mp)] = xt
-
-        def x_evac(g):
-            xg = grpp.tile([P, TOK, 4], BF16, name="xg%d" % g, tag="xg", bufs=2, align_bytes=64)
-            for mp in range(2):
-                nc.vector.tensor_copy(
-                    out=xg[:, 256 * mp:256 * (mp + 1), :].bitcast(F32),
-                    in_=xts[(g, mp)][:].rearrange("p u r -> p r u"),
-                )
-            xgs[g] = xg
 
         def x_quant(g):
             nc.vector.quantize_mx(
                 out=xc[:, g, :].bitcast(FP8X4),
                 scales=xs[:, g, :],
-                in_=xgs[g][:].rearrange("p r j -> p (r j)"),
+                in_=xg[:, g, :, :].rearrange("p r j -> p (r j)"),
             )
 
         def inter_v(q):
             grp[q] = grpp.tile([P, NW, 4], BF16, name="grp%d" % q, tag="grpv", bufs=3, align_bytes=64)
-            nc.vector.tensor_copy(
-                out=grp[q][:].rearrange("p (c i) j -> p c j i", i=4),
-                in_=raw[q][:].rearrange("p j (c i) -> p c j i", i=4),
-            )
+            nc.vector.tensor_copy(out=grp[q][:], in_=raw[q][:].rearrange("p j w -> p w j"))
+
+        def inter_v_odd(q):
+            if q == 7:
+                grp[q] = grpp.tile([P, NW, 4], BF16, name="grp%d" % q, tag="grpg", bufs=1, align_bytes=64)
+            else:
+                grp[q] = grpp.tile([P, NW, 4], BF16, name="grp%d" % q, tag="grpv", bufs=3, align_bytes=64)
+            nc.vector.tensor_copy(out=grp[q][:], in_=raw[q][:].rearrange("p j w -> p w j"))
 
         def inter_g(q):
             grp[q] = grpp.tile([P, NW, 4], BF16, name="grp%d" % q, tag="grpg", bufs=1, align_bytes=64)
@@ -261,10 +258,7 @@ def tile_yatnmn_kernel(tc, x, kernel, bias, alpha, out_0, out_1):
         def addb(s):
             nb, m = divmod(s, NM)
             cols = slice(NW * nb, NW * (nb + 1))
-            if G_ADD_FIRST <= s <= G_ADD_LAST:
-                nc.gpsimd.tensor_tensor(out=out_sb[:, m, cols], in0=t2s[s][:], in1=b_c[:, cols], op=ALU.add)
-            else:
-                nc.vector.tensor_tensor(out=out_sb[:, m, cols], in0=t2s[s][:], in1=b_c[:, cols], op=ALU.add)
+            nc.vector.tensor_tensor(out=out_sb[:, m, cols], in0=t2s[s][:], in1=b_c[:, cols], op=ALU.add)
             nc.sync.dma_start(out=o0[P * m:P * (m + 1), cols], in_=out_sb[:, m, cols])
 
         def absmax(s):
@@ -275,14 +269,13 @@ def tile_yatnmn_kernel(tc, x, kernel, bias, alpha, out_0, out_1):
             )
 
         nc.scalar.dma_start(out=alpha_t[:], in_=alpha.partition_broadcast(P))
-        load_raw(0)
-        load_raw(1)
         for m in range(NM):
             load_x(m)
-        for q in range(2, 6):
+            load_raw(m)
+        for q in range(4, 7):
             load_raw(q)
-        load_bias(0)
-        load_bias(1)
+        xg = grpp.tile([P, NG, TOK, 4], BF16, name="xg", tag="xg", bufs=1, align_bytes=64)
+        gx = psm.tile([P, NW], F32, name="gx", tag="misc")
 
         make_identity(nc, ident_f[:])
         make_identity(nc, ident_bf[:])
@@ -298,7 +291,9 @@ def tile_yatnmn_kernel(tc, x, kernel, bias, alpha, out_0, out_1):
             return 0 <= t < 2 * NSTEP
 
         def scale_bias(h):
-            nc.scalar.activation(out=b_c[:, D * h:D * (h + 1)], in_=stg[h][:], func=ACT.Copy, scale=c_t[:, 0:1])
+            nc.vector.tensor_scalar(
+                out=b_c[:, D * h:D * (h + 1)], in0=stg[h][:], scalar1=c_t[:, 0:1], scalar2=None, op0=ALU.mult
+            )
 
         with tc.manual_schedule():
             for k in range(-4, 18):
@@ -306,12 +301,19 @@ def tile_yatnmn_kernel(tc, x, kernel, bias, alpha, out_0, out_1):
                 due = (k + 1) % 2 == 0 and 0 <= (k + 1) // 2 < NB
                 nbd = (k + 1) // 2
                 for q in (2 * k + 12, 2 * k + 13):
-                    if 6 <= q < NSTEP:
+                    if 7 <= q < NSTEP:
                         load_raw(q)
+                if k == -2:
+                    load_bias(0)
+                    load_bias(1)
+                if k == -4:
+                    x_trans(0)
+                    x_trans(1)
+                if k == -3 or k == -2:
+                    x_gram(2 * k + 6)
+                    x_gram(2 * k + 7)
                 if ok(2 * k + 1):
                     mx(2 * k + 1)
-                if ok(2 * k + 2):
-                    mx(2 * k + 2)
                 if due:
                     ksq_reduce(nbd)
                     ksq_bcast(nbd)
@@ -319,25 +321,48 @@ def tile_yatnmn_kernel(tc, x, kernel, bias, alpha, out_0, out_1):
                     square(2 * k - 2)
                 if okt(t0 + 3):
                     ktrans(t0 + 3)
+                if k == -3:
+                    x_trans(2)
+                    x_trans(3)
                 for t in (t0, t0 + 1, t0 + 2):
                     if okt(t):
                         ksq_act(t)
                 if ok(2 * k + 8):
                     inter_v(2 * k + 8)
+                if k == -4:
+                    x_evac(0)
                 if ok(2 * k - 3):
                     addb(2 * k - 3)
-                if k == -3 or k == -2:
-                    x_quant(2 * k + 6)
+                if k == -2:
+                    x_quant(0)
+                if k == 0 or k == 1:
+                    scale_bias(k)
                 if ok(2 * k + 6):
                     quant(2 * k + 6)
+                if k == -3:
+                    x_evac(2)
                 if ok(2 * k - 2):
                     addb(2 * k - 2)
-                if k == -3 or k == -2:
-                    x_quant(2 * k + 7)
+                if k == -2:
+                    x_quant(1)
                 if ok(2 * k + 7):
                     quant(2 * k + 7)
                 if ok(2 * k + 9):
-                    inter_g(2 * k + 9)
+                    if 2 * k + 9 <= 7:
+                        inter_v_odd(2 * k + 9)
+                    else:
+                        inter_g(2 * k + 9)
+                if k == -4:
+                    x_evac(1)
+                if k == -3:
+                    x_evac(3)
+                if k == -2:
+                    x_quant(2)
+                    x_quant(3)
+                    x_diag()
+                    nc.vector.tensor_scalar(out=xsqe[:], in0=xsq[:], scalar1=EPS, scalar2=None, op0=ALU.add)
+                if ok(2 * k + 2):
+                    mx(2 * k + 2)
                 for t in (t0 + 4, t0 + 5):
                     if okt(t):
                         ktrans(t)
@@ -353,9 +378,6 @@ def tile_yatnmn_kernel(tc, x, kernel, bias, alpha, out_0, out_1):
                     absmax(2 * k - 3)
                 if okt(t0 + 3):
                     ksq_act(t0 + 3)
-                if k == -1:
-                    scale_bias(0)
-                    scale_bias(1)
                 if ok(2 * k + 1):
                     dprime(2 * k + 1)
                     ars(2 * k + 1)
@@ -365,17 +387,6 @@ def tile_yatnmn_kernel(tc, x, kernel, bias, alpha, out_0, out_1):
                     umul(2 * k)
                 if okt(t0 + 6):
                     ktrans(t0 + 6)
-                if k == -4 or k == -3:
-                    ga = 2 * k + 8
-                    x_trans(ga)
-                    x_trans(ga + 1)
-                    x_evac(ga)
-                    x_evac(ga + 1)
-                    x_gram(ga)
-                    x_gram(ga + 1)
-                if k == -2:
-                    x_diag()
-                    nc.vector.tensor_scalar(out=xsqe[:], in0=xsq[:], scalar1=EPS, scalar2=None, op0=ALU.add)
 
         nc.vector.tensor_reduce(out=pmax[:], in_=amax_cols[:], axis=AX.X, op=ALU.max)
         pt = psm.tile([P, P], F32, name="pt", tag="misc")

@@ -26,6 +26,11 @@ NSTEP = NB * NM
 EPS = 1.0 / 137.0
 LOG_RATIO = math.log(math.sqrt(4096.0) / math.log(1.0 + 4096.0))
 CV = 1408
+PASS_ORDER = (2, 3, 0, 1)
+GRP_TAG = ("g0", "gA", "gB", "gC")
+GRAM = (2, 1, 2, 1, 2, 1, 2, 1)
+CS = 192
+CG = 192
 
 FLOPS = 2 * TOK * D * O
 
@@ -38,29 +43,30 @@ def tile_yatnmn_kernel(tc, x, kernel, bias, alpha, out_0, out_1):
 
     with ExitStack() as ctx:
         keep = ctx.enter_context(tc.tile_pool(name="keep", bufs=1))
-        rawp = ctx.enter_context(tc.tile_pool(name="rawp", bufs=11))
-        grpp = ctx.enter_context(tc.tile_pool(name="grpp", bufs=3))
-        codp = ctx.enter_context(tc.tile_pool(name="codp", bufs=10))
+        rawp = ctx.enter_context(tc.tile_pool(name="rawp", bufs=12))
+        grpp = ctx.enter_context(tc.tile_pool(name="grpp", bufs=1))
+        codp = ctx.enter_context(tc.tile_pool(name="codp", bufs=8))
         tmpp = ctx.enter_context(tc.tile_pool(name="tmpp", bufs=4))
         smlp = ctx.enter_context(tc.tile_pool(name="smlp", bufs=2))
         psy = ctx.enter_context(tc.psum_pool(name="psy", bufs=4))
-        psk = ctx.enter_context(tc.psum_pool(name="psk", bufs=3))
+        psk = ctx.enter_context(tc.psum_pool(name="psk", bufs=2))
+        psc = ctx.enter_context(tc.psum_pool(name="psc", bufs=1))
         psm = ctx.enter_context(tc.psum_pool(name="psm", bufs=1))
 
         out_sb = keep.tile([P, NM, O], F32, name="out_sb")
         q8 = keep.tile([P, NM, O], FP8, name="q8")
-        b_c = keep.tile([P, O], F32, name="b_c")
-        xc = keep.tile([P, NG, TOK], U32, name="xc", align_bytes=64)
-        xs = keep.tile([P, NG, TOK], U8, name="xs", align_bytes=64)
+        xc = keep.tile([P, NM, NG * P], U32, name="xc", align_bytes=64)
+        xs = keep.tile([P, NM, NG * P], U8, name="xs", align_bytes=64)
         ident_bf = keep.tile([P, P], BF16, name="ident_bf")
         ident_f = keep.tile([P, P], F32, name="ident_f")
+        bias_rows = keep.tile([P, P], BF16, name="bias_rows")
+        cbcol = keep.tile([P, O // P], F32, name="cbcol")
         alpha_t = keep.tile([P, 1], BF16, name="alpha_t")
         c_t = keep.tile([P, 1], F32, name="c_t")
         sc_t = keep.tile([P, 1], F32, name="sc_t")
         dummy = keep.tile([P, 1], F32, name="dummy")
         zero = keep.tile([P, 1], F32, name="zero")
         xsq = keep.tile([P, NM], F32, name="xsq")
-        xsqe = keep.tile([P, NM], F32, name="xsqe")
         ksq_cols = keep.tile([P, 2 * NSTEP], F32, name="ksq_cols")
         amax_cols = keep.tile([P, NSTEP], F32, name="amax_cols")
         pmax = keep.tile([P, 1], F32, name="pmax")
@@ -73,17 +79,24 @@ def tile_yatnmn_kernel(tc, x, kernel, bias, alpha, out_0, out_1):
         kc = {}
         ks = {}
         kts = {}
+        gks = {}
         k4s = {}
         kbs = {}
         ksbs = {}
+        cbs = {}
         ys = {}
         t1s = {}
         t2s = {}
         xsb = {}
         xts = {}
         xgs = {}
-        stg = {}
-        gxs = {}
+
+        stream = []
+        for nb in range(NB):
+            for h in range(2):
+                for ob in range(GRAM[nb], 4):
+                    stream.append((nb, h, ob))
+        state = {"fill": 0, "act": 0, "mx": 0, "kq": -1, "xq": -1}
 
         def load_raw(q):
             nb, g = divmod(q, NG)
@@ -99,11 +112,6 @@ def tile_yatnmn_kernel(tc, x, kernel, bias, alpha, out_0, out_1):
             nc.sync.dma_start(out=t[:], in_=xf[P * m:P * (m + 1), :])
             xsb[m] = t
 
-        def load_bias(h):
-            t = rawp.tile([P, D], BF16, name="stg%d" % h, tag="raw")
-            nc.sync.dma_start(out=t[:], in_=bias[D * h:D * (h + 1)].partition_broadcast(P))
-            stg[h] = t
-
         def x_trans(m):
             words = xsb[m][:].bitcast(F32)
             for gp in range(2):
@@ -117,52 +125,56 @@ def tile_yatnmn_kernel(tc, x, kernel, bias, alpha, out_0, out_1):
                 xts[(m, gp)] = xt
 
         def x_evac(m):
+            xgs[m] = grpp.tile([P, NG, P, 4], BF16, name="xg%d" % m, tag="xg", bufs=2, align_bytes=64)
             for gp in range(2):
                 nc.vector.tensor_copy(
-                    out=xg[:, 2 * gp:2 * gp + 2, P * m:P * (m + 1), :].bitcast(F32),
+                    out=xgs[m][:, 2 * gp:2 * gp + 2, :, :].bitcast(F32),
                     in_=xts[(m, gp)][:].rearrange("p g u r -> p g r u"),
                 )
 
-        def x_gram(m):
-            for g in range(NG):
-                for j in range(4):
-                    xt_mj = xg[:, g, P * m:P * (m + 1), j]
-                    nc.tensor.matmul(
-                        out=gx[:, P * m:P * (m + 1)], lhsT=xt_mj, rhs=xt_mj,
-                        start=(g == 0 and j == 0), stop=(g == NG - 1 and j == 3),
-                    )
+        def x_square(m):
+            junk = smlp.tile([P, D], BF16, name="junkx%d" % m, tag="junk")
+            nc.scalar.activation(out=junk[:], in_=xsb[m][:], func=ACT.Square, accum_out=xsq[:, m:m + 1])
 
-        def x_diag():
-            for m in range(NM):
-                junkf = tmpp.tile([P, P], F32, name="junkf%d" % m, tag="t1")
-                nc.vector.scalar_tensor_tensor(
-                    out=junkf[:], in0=gx[:, P * m:P * (m + 1)], scalar=1.0, in1=ident_f[:], op0=ALU.mult,
-                    op1=ALU.mult, accum_out=xsq[:, m:m + 1],
-                )
-
-        def x_quant(g):
+        def x_quant(m):
             nc.vector.quantize_mx(
-                out=xc[:, g, :].bitcast(FP8X4),
-                scales=xs[:, g, :],
-                in_=xg[:, g, :, :].rearrange("p r j -> p (r j)"),
+                out=xc[:, m, :].bitcast(FP8X4),
+                scales=xs[:, m, :],
+                in_=xgs[m][:].rearrange("p g r j -> p (g r j)"),
             )
+            state["xq"] = m
+
+        def new_grp(q):
+            grp[q] = grpp.tile([P, NW, 4], BF16, name="grp%d" % q, tag=GRP_TAG[q % NG], bufs=1, align_bytes=64)
 
         def inter_v(q):
-            grp[q] = grpp.tile([P, NW, 4], BF16, name="grp%d" % q, tag="grpv", bufs=3, align_bytes=64)
-            nc.vector.tensor_copy(out=grp[q][:], in_=raw[q][:].rearrange("p j w -> p w j"))
-
-        def inter_v_odd(q):
-            if q == 7:
-                grp[q] = grpp.tile([P, NW, 4], BF16, name="grp%d" % q, tag="grpg", bufs=1, align_bytes=64)
-            else:
-                grp[q] = grpp.tile([P, NW, 4], BF16, name="grp%d" % q, tag="grpv", bufs=3, align_bytes=64)
+            new_grp(q)
             nc.vector.tensor_copy(out=grp[q][:], in_=raw[q][:].rearrange("p j w -> p w j"))
 
         def inter_g(q):
-            grp[q] = grpp.tile([P, NW, 4], BF16, name="grp%d" % q, tag="grpg", bufs=1, align_bytes=64)
+            new_grp(q)
             nc.gpsimd.tensor_scalar(
                 out=grp[q][:], in0=raw[q][:].rearrange("p j w -> p w j"), scalar1=1.0, scalar2=0.0,
                 op0=ALU.mult, op1=ALU.add,
+            )
+
+        def inter_s(q):
+            new_grp(q)
+            nc.scalar.copy(out=grp[q][:, 0:CS, :], in_=raw[q][:, :, 0:CS].rearrange("p j w -> p w j"))
+
+        def inter_s_whole(q):
+            new_grp(q)
+            nc.scalar.copy(out=grp[q][:], in_=raw[q][:].rearrange("p j w -> p w j"))
+
+        def inter_g_rest(q):
+            nc.gpsimd.tensor_scalar(
+                out=grp[q][:, CS:CS + CG, :], in0=raw[q][:, :, CS:CS + CG].rearrange("p j w -> p w j"),
+                scalar1=1.0, scalar2=0.0, op0=ALU.mult, op1=ALU.add,
+            )
+
+        def inter_v_rest(q):
+            nc.vector.tensor_copy(
+                out=grp[q][:, CS + CG:NW, :], in_=raw[q][:, :, CS + CG:NW].rearrange("p j w -> p w j")
             )
 
         def quant(q):
@@ -171,10 +183,15 @@ def tile_yatnmn_kernel(tc, x, kernel, bias, alpha, out_0, out_1):
             nc.vector.quantize_mx(out=c[:].bitcast(FP8X4), scales=s[:], in_=grp[q][:].rearrange("p w j -> p (w j)"))
             kc[q] = c
             ks[q] = s
+            if q % NG == PASS_ORDER[3]:
+                state["kq"] = q // NG
 
-        def ktrans(t):
-            nb, r = divmod(t, 8)
-            h, ob = divmod(r, 4)
+        def fill():
+            t = state["fill"]
+            if t >= len(stream):
+                return
+            state["fill"] = t + 1
+            nb, h, ob = stream[t]
             kt = psk.tile([P, 8 * P], BF16, name="kt%d" % t, tag="kT")
             for i in range(8):
                 g = 2 * h + i // 4
@@ -186,12 +203,35 @@ def tile_yatnmn_kernel(tc, x, kernel, bias, alpha, out_0, out_1):
                 )
             kts[t] = kt
 
-        def ksq_act(t):
-            nb, r = divmod(t, 8)
-            h, ob = divmod(r, 4)
+        def act():
+            t = state["act"]
+            if t >= len(stream):
+                return
+            state["act"] = t + 1
+            nb, h, ob = stream[t]
             col = 8 * nb + 2 * ob + h
             junk = smlp.tile([P, 8 * P], BF16, name="junk%d" % t, tag="junk")
             nc.scalar.activation(out=junk[:], in_=kts[t][:], func=ACT.Square, accum_out=ksq_cols[:, col:col + 1])
+
+        def gram(nb):
+            gk = psm.tile([P, GRAM[nb], P], F32, name="gk%d" % nb, tag="misc")
+            for ob in range(GRAM[nb]):
+                for g in range(NG):
+                    for j in range(4):
+                        kk = raw[NG * nb + g][:, j, P * ob:P * (ob + 1)]
+                        nc.tensor.matmul(
+                            out=gk[:, ob, :], lhsT=kk, rhs=kk, start=(g == 0 and j == 0), stop=(g == NG - 1 and j == 3)
+                        )
+            gks[nb] = gk
+
+        def diag(nb):
+            for ob in range(GRAM[nb]):
+                junkf = tmpp.tile([P, P], F32, name="junkg%d_%d" % (nb, ob), tag="jf", bufs=2)
+                col = 8 * nb + 2 * ob
+                nc.vector.scalar_tensor_tensor(
+                    out=junkf[:], in0=gks[nb][:, ob, :], scalar=1.0, in1=ident_f[:], op0=ALU.mult,
+                    op1=ALU.mult, accum_out=ksq_cols[:, col:col + 1],
+                )
 
         def ksq_reduce(nb):
             k4 = smlp.tile([P, 4], F32, name="k4_%d" % nb, tag="k4")
@@ -215,23 +255,33 @@ def tile_yatnmn_kernel(tc, x, kernel, bias, alpha, out_0, out_1):
 
         def ksq_evac(nb):
             ksb = smlp.tile([P, NW], F32, name="ksb%d" % nb, tag="ksb")
-            nc.scalar.copy(out=ksb[:], in_=kbs[nb][:])
+            nc.scalar.activation(out=ksb[:], in_=kbs[nb][:], func=ACT.Copy, bias=EPS, scale=1.0)
             ksbs[nb] = ksb
+
+        def cb_bcast(nb):
+            cb = psc.tile([P, NW], F32, name="cb%d" % nb, tag="cb")
+            for ob in range(4):
+                i = 4 * nb + ob
+                nc.tensor.transpose(
+                    out=cb[:, P * ob:P * (ob + 1)],
+                    in_=cbcol[:, i:i + 1].to_broadcast([P, P]),
+                    identity=ident_f[:],
+                )
+            cbs[nb] = cb
 
         def mx(s):
             nb, m = divmod(s, NM)
-            y = psy.tile([P, NW], F32, name="y%d" % s, tag="y")
-            for g in range(NG):
+            ys[s] = psy.tile([P, NW], F32, name="y%d" % s, tag="y")
+            for g in PASS_ORDER:
                 nc.tensor.matmul_mx(
-                    out=y[:],
-                    lhsT=xc[:, g, P * m:P * (m + 1)].bitcast(FP8X4),
-                    lhsT_scale=xs[:, g, P * m:P * (m + 1)],
+                    out=ys[s][:],
+                    lhsT=xc[:, m, P * g:P * (g + 1)].bitcast(FP8X4),
+                    lhsT_scale=xs[:, m, P * g:P * (g + 1)],
                     rhs=kc[NG * nb + g][:].bitcast(FP8X4),
                     rhs_scale=ks[NG * nb + g][:],
-                    start=(g == 0),
-                    stop=(g == NG - 1),
+                    start=(g == PASS_ORDER[0]),
+                    stop=(g == PASS_ORDER[3]),
                 )
-            ys[s] = y
 
         def dprime(s):
             nb, m = divmod(s, NM)
@@ -240,25 +290,20 @@ def tile_yatnmn_kernel(tc, x, kernel, bias, alpha, out_0, out_1):
                 out=t1[:], in0=ys[s][:], scalar=-2.0, in1=ksbs[nb][:], op0=ALU.mult, op1=ALU.add
             )
             t1s[s] = t1
-
-        def ars(s):
-            nb, m = divmod(s, NM)
             nc.scalar.activation(
-                out=t1s[s][:], in_=t1s[s][:], func=ACT.Abs_reciprocal_sqrt, bias=xsqe[:, m:m + 1], scale=1.0
+                out=t1[:], in_=t1[:], func=ACT.Abs_reciprocal_sqrt, bias=xsq[:, m:m + 1], scale=1.0
             )
 
         def umul(s):
             t2 = tmpp.tile([P, NW], F32, name="t2_%d" % s, tag="t2")
             nc.vector.tensor_tensor(out=t2[:], in0=ys[s][:], in1=t1s[s][:], op=ALU.mult)
             t2s[s] = t2
-
-        def square(s):
-            nc.scalar.activation(out=t2s[s][:], in_=t2s[s][:], func=ACT.Square, scale=sc_t[:, 0:1])
+            nc.scalar.activation(out=t2[:], in_=t2[:], func=ACT.Square, scale=sc_t[:, 0:1])
 
         def addb(s):
             nb, m = divmod(s, NM)
             cols = slice(NW * nb, NW * (nb + 1))
-            nc.vector.tensor_tensor(out=out_sb[:, m, cols], in0=t2s[s][:], in1=b_c[:, cols], op=ALU.add)
+            nc.vector.tensor_tensor(out=out_sb[:, m, cols], in0=t2s[s][:], in1=cbs[nb][:], op=ALU.add)
             nc.sync.dma_start(out=o0[P * m:P * (m + 1), cols], in_=out_sb[:, m, cols])
 
         def absmax(s):
@@ -268,125 +313,135 @@ def tile_yatnmn_kernel(tc, x, kernel, bias, alpha, out_0, out_1):
                 axis=AX.X, op=ALU.max, apply_absolute_value=True,
             )
 
+        def ok(s):
+            return 0 <= s < NSTEP
+
+        def issue_mx(last):
+            while state["mx"] <= min(last, NSTEP - 1):
+                s = state["mx"]
+                if s // NM > state["kq"] or (s < NM and s > state["xq"]):
+                    return
+                mx(s)
+                state["mx"] = s + 1
+
+        def step(t, with_act):
+            issue_mx(t + 2)
+            if ok(t):
+                dprime(t)
+            if with_act:
+                act()
+                fill()
+            if ok(t - 3):
+                absmax(t - 3)
+            if ok(t - 1):
+                umul(t - 1)
+            if ok(t - 2):
+                addb(t - 2)
+
         nc.scalar.dma_start(out=alpha_t[:], in_=alpha.partition_broadcast(P))
+        nc.vector.memset(bias_rows[:], 0.0)
+        nc.scalar.dma_start(out=bias_rows[0:O // P, :], in_=bias.rearrange("(r c) -> r c", c=P))
         for m in range(NM):
             load_x(m)
-            load_raw(m)
-        for q in range(4, 7):
+        for q in range(8):
             load_raw(q)
-        xg = grpp.tile([P, NG, TOK, 4], BF16, name="xg", tag="xg", bufs=1, align_bytes=64)
-        gx = psm.tile([P, NW], F32, name="gx", tag="misc")
 
         make_identity(nc, ident_f[:])
         make_identity(nc, ident_bf[:])
         nc.vector.memset(zero[:], 0.0)
+        nc.vector.memset(ksq_cols[:], 0.0)
         nc.scalar.activation(out=c_t[:], in_=alpha_t[:], func=ACT.Exp, scale=LOG_RATIO)
         nc.scalar.activation(out=sc_t[:], in_=alpha_t[:], func=ACT.Exp, scale=0.5 * LOG_RATIO)
         nc.scalar.activation(out=dummy[:], in_=c_t[:], func=ACT.Abs_reciprocal_sqrt)
 
-        def ok(s):
-            return 0 <= s < NSTEP
-
-        def okt(t):
-            return 0 <= t < 2 * NSTEP
-
-        def scale_bias(h):
-            nc.vector.tensor_scalar(
-                out=b_c[:, D * h:D * (h + 1)], in0=stg[h][:], scalar1=c_t[:, 0:1], scalar2=None, op0=ALU.mult
-            )
-
         with tc.manual_schedule():
-            for k in range(-4, 18):
-                t0 = 4 * k + 12
-                due = (k + 1) % 2 == 0 and 0 <= (k + 1) // 2 < NB
-                nbd = (k + 1) // 2
-                for q in (2 * k + 12, 2 * k + 13):
-                    if 7 <= q < NSTEP:
+            for m in range(NM):
+                x_trans(m)
+                x_square(m)
+                x_evac(m)
+                if m > 0:
+                    x_quant(m - 1)
+            bias_t = psm.tile([P, P], BF16, name="bias_t", tag="misc")
+            nc.tensor.transpose(out=bias_t[:], in_=bias_rows[:], identity=ident_bf[:])
+            nc.vector.tensor_scalar(
+                out=cbcol[:], in0=bias_t[:, 0:O // P], scalar1=c_t[:, 0:1], scalar2=None, op0=ALU.mult
+            )
+            cb_bcast(0)
+            inter_v(0)
+            x_quant(3)
+            fill()
+            fill()
+            inter_v(1)
+            quant(0)
+            act()
+            fill()
+            inter_v(2)
+            act()
+            fill()
+            quant(1)
+            inter_v(3)
+            gram(0)
+            act()
+            act()
+            fill()
+            fill()
+            diag(0)
+            ksq_reduce(0)
+            quant(2)
+            inter_s_whole(NG)
+            ksq_bcast(0)
+            ksq_evac(0)
+            quant(3)
+            issue_mx(1)
+            for q in range(8, 12):
+                load_raw(q)
+            inter_v(NG + 1)
+            act()
+            fill()
+            gram(1)
+            inter_v(NG + 2)
+            act()
+            fill()
+            inter_v(NG + 3)
+            act()
+            fill()
+            step(0, False)
+            step(1, True)
+
+            for j in range(1, NB):
+                for q in range(NG * (j + 2), NG * (j + 3)):
+                    if q < NSTEP:
                         load_raw(q)
-                if k == -2:
-                    load_bias(0)
-                    load_bias(1)
-                if k == -4:
-                    x_trans(0)
-                    x_trans(1)
-                if k == -3 or k == -2:
-                    x_gram(2 * k + 6)
-                    x_gram(2 * k + 7)
-                if ok(2 * k + 1):
-                    mx(2 * k + 1)
-                if due:
-                    ksq_reduce(nbd)
-                    ksq_bcast(nbd)
-                if ok(2 * k - 2):
-                    square(2 * k - 2)
-                if okt(t0 + 3):
-                    ktrans(t0 + 3)
-                if k == -3:
-                    x_trans(2)
-                    x_trans(3)
-                for t in (t0, t0 + 1, t0 + 2):
-                    if okt(t):
-                        ksq_act(t)
-                if ok(2 * k + 8):
-                    inter_v(2 * k + 8)
-                if k == -4:
-                    x_evac(0)
-                if ok(2 * k - 3):
-                    addb(2 * k - 3)
-                if k == -2:
-                    x_quant(0)
-                if k == 0 or k == 1:
-                    scale_bias(k)
-                if ok(2 * k + 6):
-                    quant(2 * k + 6)
-                if k == -3:
-                    x_evac(2)
-                if ok(2 * k - 2):
-                    addb(2 * k - 2)
-                if k == -2:
-                    x_quant(1)
-                if ok(2 * k + 7):
-                    quant(2 * k + 7)
-                if ok(2 * k + 9):
-                    if 2 * k + 9 <= 7:
-                        inter_v_odd(2 * k + 9)
-                    else:
-                        inter_g(2 * k + 9)
-                if k == -4:
-                    x_evac(1)
-                if k == -3:
-                    x_evac(3)
-                if k == -2:
-                    x_quant(2)
-                    x_quant(3)
-                    x_diag()
-                    nc.vector.tensor_scalar(out=xsqe[:], in0=xsq[:], scalar1=EPS, scalar2=None, op0=ALU.add)
-                if ok(2 * k + 2):
-                    mx(2 * k + 2)
-                for t in (t0 + 4, t0 + 5):
-                    if okt(t):
-                        ktrans(t)
-                if due:
-                    ksq_evac(nbd)
-                if ok(2 * k):
-                    dprime(2 * k)
-                    ars(2 * k)
-                if ok(2 * k - 1):
-                    umul(2 * k - 1)
-                    square(2 * k - 1)
-                if ok(2 * k - 3):
-                    absmax(2 * k - 3)
-                if okt(t0 + 3):
-                    ksq_act(t0 + 3)
-                if ok(2 * k + 1):
-                    dprime(2 * k + 1)
-                    ars(2 * k + 1)
-                if ok(2 * k - 2):
-                    absmax(2 * k - 2)
-                if ok(2 * k):
-                    umul(2 * k)
-                if okt(t0 + 6):
-                    ktrans(t0 + 6)
+                if j > 1:
+                    cb_bcast(j - 1)
+                    inter_v_rest(NG * j)
+                act()
+                fill()
+                quant(NG * j + 2)
+                quant(NG * j + 3)
+                quant(NG * j)
+                if j + 1 < NB:
+                    inter_s(NG * (j + 1))
+                quant(NG * j + 1)
+                if j + 1 < NB:
+                    for g in (1, 2, 3):
+                        inter_g(NG * (j + 1) + g)
+                    inter_g_rest(NG * (j + 1))
+                for t in range(4 * j - 2, 4 * j + 2):
+                    step(t, True)
+                    if t == 4 * j - 2:
+                        if j == 1:
+                            diag(1)
+                        ksq_reduce(j)
+                        ksq_bcast(j)
+                        ksq_evac(j)
+                    if t == 4 * j - 1 and j + 1 < NB:
+                        gram(j + 1)
+                    if t == 4 * j + 1 and j + 1 < NB:
+                        diag(j + 1)
+            cb_bcast(NB - 1)
+            for t in range(NSTEP - 2, NSTEP + 3):
+                step(t, False)
 
         nc.vector.tensor_reduce(out=pmax[:], in_=amax_cols[:], axis=AX.X, op=ALU.max)
         pt = psm.tile([P, P], F32, name="pt", tag="misc")

@@ -29,6 +29,8 @@ CV = 1408
 PASS_ORDER = (2, 3, 0, 1)
 GRP_TAG = ("g0", "gA", "gB", "gC")
 GRAM = (2, 1, 2, 1, 2, 1, 2, 1)
+GADD_FROM = 24
+GADD_TO = 32
 CS = 192
 CG = 192
 
@@ -84,6 +86,7 @@ def tile_yatnmn_kernel(tc, x, kernel, bias, alpha, out_0, out_1):
         kbs = {}
         ksbs = {}
         cbs = {}
+        cbsb = {}
         ys = {}
         t1s = {}
         t2s = {}
@@ -300,10 +303,18 @@ def tile_yatnmn_kernel(tc, x, kernel, bias, alpha, out_0, out_1):
             t2s[s] = t2
             nc.scalar.activation(out=t2[:], in_=t2[:], func=ACT.Square, scale=sc_t[:, 0:1])
 
+        def cb_evac(nb):
+            t = smlp.tile([P, NW], F32, name="cbsb%d" % nb, tag="cbsb")
+            nc.scalar.copy(out=t[:], in_=cbs[nb][:])
+            cbsb[nb] = t
+
         def addb(s):
             nb, m = divmod(s, NM)
             cols = slice(NW * nb, NW * (nb + 1))
-            nc.vector.tensor_tensor(out=out_sb[:, m, cols], in0=t2s[s][:], in1=cbs[nb][:], op=ALU.add)
+            if GADD_FROM <= s < GADD_TO:
+                nc.gpsimd.tensor_tensor(out=out_sb[:, m, cols], in0=t2s[s][:], in1=cbsb[nb][:], op=ALU.add)
+            else:
+                nc.vector.tensor_tensor(out=out_sb[:, m, cols], in0=t2s[s][:], in1=cbs[nb][:], op=ALU.add)
             nc.sync.dma_start(out=o0[P * m:P * (m + 1), cols], in_=out_sb[:, m, cols])
 
         def absmax(s):
@@ -417,6 +428,8 @@ def tile_yatnmn_kernel(tc, x, kernel, bias, alpha, out_0, out_1):
                     inter_v_rest(NG * j)
                 act()
                 fill()
+                if NM * (j - 1) >= GADD_FROM:
+                    cb_evac(j - 1)
                 quant(NG * j + 2)
                 quant(NG * j + 3)
                 quant(NG * j)
@@ -440,6 +453,7 @@ def tile_yatnmn_kernel(tc, x, kernel, bias, alpha, out_0, out_1):
                     if t == 4 * j + 1 and j + 1 < NB:
                         diag(j + 1)
             cb_bcast(NB - 1)
+            cb_evac(NB - 1)
             for t in range(NSTEP - 2, NSTEP + 3):
                 step(t, False)
 

@@ -30,7 +30,7 @@ PASS_ORDER = (2, 3, 0, 1)
 GRP_TAG = ("g0", "gA", "gB", "gC")
 GRAM = (2, 1, 2, 1, 2, 1, 2, 1)
 GADD_FROM = 24
-GADD_TO = 32
+GADD_TO = 31
 CS = 192
 CG = 192
 
@@ -342,12 +342,12 @@ def tile_yatnmn_kernel(tc, x, kernel, bias, alpha, out_0, out_1):
             if with_act:
                 act()
                 fill()
+            if ok(t - 4):
+                absmax(t - 4)
             if ok(t - 3):
-                absmax(t - 3)
+                addb(t - 3)
             if ok(t - 1):
                 umul(t - 1)
-            if ok(t - 2):
-                addb(t - 2)
 
         nc.scalar.dma_start(out=alpha_t[:], in_=alpha.partition_broadcast(P))
         nc.vector.memset(bias_rows[:], 0.0)
@@ -372,12 +372,6 @@ def tile_yatnmn_kernel(tc, x, kernel, bias, alpha, out_0, out_1):
                 x_evac(m)
                 if m > 0:
                     x_quant(m - 1)
-            bias_t = psm.tile([P, P], BF16, name="bias_t", tag="misc")
-            nc.tensor.transpose(out=bias_t[:], in_=bias_rows[:], identity=ident_bf[:])
-            nc.vector.tensor_scalar(
-                out=cbcol[:], in0=bias_t[:, 0:O // P], scalar1=c_t[:, 0:1], scalar2=None, op0=ALU.mult
-            )
-            cb_bcast(0)
             inter_v(0)
             x_quant(3)
             fill()
@@ -392,32 +386,45 @@ def tile_yatnmn_kernel(tc, x, kernel, bias, alpha, out_0, out_1):
             quant(1)
             inter_v(3)
             gram(0)
+            bias_t = psc.tile([P, P], BF16, name="bias_t", tag="cb")
+            nc.tensor.transpose(out=bias_t[:], in_=bias_rows[:], identity=ident_bf[:])
             act()
             act()
             fill()
             fill()
-            diag(0)
-            ksq_reduce(0)
             quant(2)
             inter_s_whole(NG)
+            act()
+            diag(0)
+            nc.vector.tensor_scalar(
+                out=cbcol[:], in0=bias_t[:, 0:O // P], scalar1=c_t[:, 0:1], scalar2=None, op0=ALU.mult
+            )
+            quant(3)
+            ksq_reduce(0)
             ksq_bcast(0)
             ksq_evac(0)
-            quant(3)
+            issue_mx(0)
+            fill()
             issue_mx(1)
             for q in range(8, 12):
                 load_raw(q)
             inter_v(NG + 1)
             act()
             fill()
-            gram(1)
+            cb_bcast(0)
+            issue_mx(2)
             inter_v(NG + 2)
             act()
             fill()
+            gram(1)
+            issue_mx(3)
             inter_v(NG + 3)
-            act()
-            fill()
             step(0, False)
             step(1, True)
+            step(2, True)
+            act()
+            fill()
+            diag(1)
 
             for j in range(1, NB):
                 for q in range(NG * (j + 2), NG * (j + 3)):
@@ -430,32 +437,46 @@ def tile_yatnmn_kernel(tc, x, kernel, bias, alpha, out_0, out_1):
                 fill()
                 if NM * (j - 1) >= GADD_FROM:
                     cb_evac(j - 1)
+                    cb_bcast(j)
+                    cb_evac(j)
                 quant(NG * j + 2)
                 quant(NG * j + 3)
+                if j > 1:
+                    ksq_reduce(j)
+                    ksq_bcast(j)
                 quant(NG * j)
                 if j + 1 < NB:
                     inter_s(NG * (j + 1))
+                if j > 1:
+                    ksq_evac(j)
                 quant(NG * j + 1)
+                if j == 1:
+                    ksq_reduce(j)
+                    ksq_bcast(j)
+                    ksq_evac(j)
                 if j + 1 < NB:
                     for g in (1, 2, 3):
                         inter_g(NG * (j + 1) + g)
                     inter_g_rest(NG * (j + 1))
-                for t in range(4 * j - 2, 4 * j + 2):
+                issue_mx(4 * j + 1)
+                if j + 1 < NB:
+                    gram(j + 1)
+                for t in range(4 * j - 1, 4 * j + 3):
                     step(t, True)
-                    if t == 4 * j - 2:
-                        if j == 1:
-                            diag(1)
-                        ksq_reduce(j)
-                        ksq_bcast(j)
-                        ksq_evac(j)
-                    if t == 4 * j - 1 and j + 1 < NB:
-                        gram(j + 1)
                     if t == 4 * j + 1 and j + 1 < NB:
                         diag(j + 1)
-            cb_bcast(NB - 1)
-            cb_evac(NB - 1)
-            for t in range(NSTEP - 2, NSTEP + 3):
-                step(t, False)
+            dprime(NSTEP - 1)
+            umul(NSTEP - 2)
+            absmax(NSTEP - 5)
+            addb(NSTEP - 4)
+            absmax(NSTEP - 4)
+            umul(NSTEP - 1)
+            addb(NSTEP - 3)
+            absmax(NSTEP - 3)
+            addb(NSTEP - 2)
+            absmax(NSTEP - 2)
+            addb(NSTEP - 1)
+            absmax(NSTEP - 1)
 
         nc.vector.tensor_reduce(out=pmax[:], in_=amax_cols[:], axis=AX.X, op=ALU.max)
         pt = psm.tile([P, P], F32, name="pt", tag="misc")

@@ -216,16 +216,19 @@ def tile_yatnmn_kernel(tc, x, kernel, bias, alpha, out_0, out_1):
             junk = smlp.tile([P, 8 * P], BF16, name="junk%d" % t, tag="junk")
             nc.scalar.activation(out=junk[:], in_=kts[t][:], func=ACT.Square, accum_out=ksq_cols[:, col:col + 1])
 
-        def gram(nb):
-            gk = psm.tile([P, GRAM[nb], P], F32, name="gk%d" % nb, tag="misc")
-            for ob in range(GRAM[nb]):
+        def gram(nb, tiles):
+            if 0 in tiles:
+                gks[nb] = psm.tile([P, GRAM[nb], P], F32, name="gk%d" % nb, tag="misc")
+            gk = gks[nb]
+            for ob in tiles:
+                if ob >= GRAM[nb]:
+                    continue
                 for g in range(NG):
                     for j in range(4):
                         kk = raw[NG * nb + g][:, j, P * ob:P * (ob + 1)]
                         nc.tensor.matmul(
                             out=gk[:, ob, :], lhsT=kk, rhs=kk, start=(g == 0 and j == 0), stop=(g == NG - 1 and j == 3)
                         )
-            gks[nb] = gk
 
         def diag(nb):
             for ob in range(GRAM[nb]):
@@ -385,7 +388,7 @@ def tile_yatnmn_kernel(tc, x, kernel, bias, alpha, out_0, out_1):
             fill()
             quant(1)
             inter_v(3)
-            gram(0)
+            gram(0, (0, 1))
             bias_t = psc.tile([P, P], BF16, name="bias_t", tag="cb")
             nc.tensor.transpose(out=bias_t[:], in_=bias_rows[:], identity=ident_bf[:])
             act()
@@ -400,23 +403,23 @@ def tile_yatnmn_kernel(tc, x, kernel, bias, alpha, out_0, out_1):
                 out=cbcol[:], in0=bias_t[:, 0:O // P], scalar1=c_t[:, 0:1], scalar2=None, op0=ALU.mult
             )
             quant(3)
-            ksq_reduce(0)
-            ksq_bcast(0)
-            ksq_evac(0)
             issue_mx(0)
+            ksq_reduce(0)
+            act()
+            ksq_bcast(0)
             fill()
+            ksq_evac(0)
             issue_mx(1)
+            fill()
             for q in range(8, 12):
                 load_raw(q)
             inter_v(NG + 1)
             act()
-            fill()
             cb_bcast(0)
             issue_mx(2)
-            inter_v(NG + 2)
-            act()
             fill()
-            gram(1)
+            inter_v(NG + 2)
+            gram(1, (0, 1))
             issue_mx(3)
             inter_v(NG + 3)
             step(0, False)
@@ -434,16 +437,15 @@ def tile_yatnmn_kernel(tc, x, kernel, bias, alpha, out_0, out_1):
                     cb_bcast(j - 1)
                     inter_v_rest(NG * j)
                 act()
-                fill()
                 if NM * (j - 1) >= GADD_FROM:
                     cb_evac(j - 1)
                     cb_bcast(j)
                     cb_evac(j)
                 quant(NG * j + 2)
-                quant(NG * j + 3)
                 if j > 1:
                     ksq_reduce(j)
                     ksq_bcast(j)
+                quant(NG * j + 3)
                 quant(NG * j)
                 if j + 1 < NB:
                     inter_s(NG * (j + 1))
@@ -458,12 +460,16 @@ def tile_yatnmn_kernel(tc, x, kernel, bias, alpha, out_0, out_1):
                     for g in (1, 2, 3):
                         inter_g(NG * (j + 1) + g)
                     inter_g_rest(NG * (j + 1))
+                issue_mx(4 * j)
+                fill()
                 issue_mx(4 * j + 1)
                 if j + 1 < NB:
-                    gram(j + 1)
+                    gram(j + 1, (0,))
                 for t in range(4 * j - 1, 4 * j + 3):
                     step(t, True)
-                    if t == 4 * j + 1 and j + 1 < NB:
+                    if t == 4 * j and j + 1 < NB:
+                        gram(j + 1, (1,))
+                    if t == 4 * j + 2 and j + 1 < NB:
                         diag(j + 1)
             dprime(NSTEP - 1)
             umul(NSTEP - 2)

@@ -28,7 +28,7 @@ LOG_RATIO = math.log(math.sqrt(4096.0) / math.log(1.0 + 4096.0))
 CV = 1408
 PASS_ORDER = (2, 3, 0, 1)
 GRP_TAG = ("g0", "gA", "gB", "gC")
-GRAM = (2, 1, 2, 1, 2, 1, 2, 1)
+GRAM = (2, 2, 2, 0, 2, 2, 2, 0)
 GADD_FROM = 24
 GADD_TO = 31
 CS = 192
@@ -69,7 +69,7 @@ def tile_yatnmn_kernel(tc, x, kernel, bias, alpha, out_0, out_1):
         dummy = keep.tile([P, 1], F32, name="dummy")
         zero = keep.tile([P, 1], F32, name="zero")
         xsq = keep.tile([P, NM], F32, name="xsq")
-        ksq_cols = keep.tile([P, 2 * NSTEP], F32, name="ksq_cols")
+        ksq_cols = keep.tile([P, 16 * NB], F32, name="ksq_cols")
         amax_cols = keep.tile([P, NSTEP], F32, name="amax_cols")
         pmax = keep.tile([P, 1], F32, name="pmax")
         amax = keep.tile([P, 1], F32, name="amax")
@@ -96,9 +96,9 @@ def tile_yatnmn_kernel(tc, x, kernel, bias, alpha, out_0, out_1):
 
         stream = []
         for nb in range(NB):
-            for h in range(2):
-                for ob in range(GRAM[nb], 4):
-                    stream.append((nb, h, ob))
+            for g in range(NG):
+                for c in range(GRAM[nb] // 2, 2):
+                    stream.append((nb, c, g))
         state = {"fill": 0, "act": 0, "mx": 0, "kq": -1, "xq": -1}
 
         def load_raw(q):
@@ -194,16 +194,11 @@ def tile_yatnmn_kernel(tc, x, kernel, bias, alpha, out_0, out_1):
             if t >= len(stream):
                 return
             state["fill"] = t + 1
-            nb, h, ob = stream[t]
-            kt = psk.tile([P, 8 * P], BF16, name="kt%d" % t, tag="kT")
-            for i in range(8):
-                g = 2 * h + i // 4
-                j = i % 4
-                nc.tensor.transpose(
-                    out=kt[:, P * i:P * (i + 1)],
-                    in_=raw[NG * nb + g][:, j, P * ob:P * (ob + 1)],
-                    identity=ident_bf[:],
-                )
+            nb, c, g = stream[t]
+            kt = psk.tile([P, 4, P], F32, name="kt%d" % t, tag="kT")
+            words = raw[NG * nb + g][:].bitcast(F32)
+            for j in range(4):
+                nc.tensor.transpose(out=kt[:, j, :], in_=words[:, j, P * c:P * (c + 1)], identity=ident_f[:])
             kts[t] = kt
 
         def act():
@@ -211,12 +206,18 @@ def tile_yatnmn_kernel(tc, x, kernel, bias, alpha, out_0, out_1):
             if t >= len(stream):
                 return
             state["act"] = t + 1
-            nb, h, ob = stream[t]
-            col = 8 * nb + 2 * ob + h
-            junk = smlp.tile([P, 8 * P], BF16, name="junk%d" % t, tag="junk")
-            nc.scalar.activation(out=junk[:], in_=kts[t][:], func=ACT.Square, accum_out=ksq_cols[:, col:col + 1])
+            nb, c, g = stream[t]
+            halves = kts[t][:].rearrange("p j q -> p (j q)").bitcast(BF16).rearrange("p (n e) -> p n e", e=2)
+            for e in range(2):
+                col = 16 * nb + 8 * c + 4 * e + g
+                junk = smlp.tile([P, 4 * P], BF16, name="junk%d_%d" % (t, e), tag="junk")
+                nc.scalar.activation(
+                    out=junk[:], in_=halves[:, :, e], func=ACT.Square, accum_out=ksq_cols[:, col:col + 1]
+                )
 
         def gram(nb, tiles):
+            if GRAM[nb] == 0:
+                return
             if 0 in tiles:
                 gks[nb] = psm.tile([P, GRAM[nb], P], F32, name="gk%d" % nb, tag="misc")
             gk = gks[nb]
@@ -233,7 +234,7 @@ def tile_yatnmn_kernel(tc, x, kernel, bias, alpha, out_0, out_1):
         def diag(nb):
             for ob in range(GRAM[nb]):
                 junkf = tmpp.tile([P, P], F32, name="junkg%d_%d" % (nb, ob), tag="jf", bufs=2)
-                col = 8 * nb + 2 * ob
+                col = 16 * nb + 4 * ob
                 nc.vector.scalar_tensor_tensor(
                     out=junkf[:], in0=gks[nb][:, ob, :], scalar=1.0, in1=ident_f[:], op0=ALU.mult,
                     op1=ALU.mult, accum_out=ksq_cols[:, col:col + 1],
@@ -243,7 +244,7 @@ def tile_yatnmn_kernel(tc, x, kernel, bias, alpha, out_0, out_1):
             k4 = smlp.tile([P, 4], F32, name="k4_%d" % nb, tag="k4")
             nc.vector.tensor_reduce(
                 out=k4[:],
-                in_=ksq_cols[:, 8 * nb:8 * (nb + 1)].rearrange("p (o h) -> p o h", h=2),
+                in_=ksq_cols[:, 16 * nb:16 * (nb + 1)].rearrange("p (o h) -> p o h", h=4),
                 axis=AX.X,
                 op=ALU.add,
             )
@@ -261,7 +262,16 @@ def tile_yatnmn_kernel(tc, x, kernel, bias, alpha, out_0, out_1):
 
         def ksq_evac(nb):
             ksb = smlp.tile([P, NW], F32, name="ksb%d" % nb, tag="ksb")
-            nc.scalar.activation(out=ksb[:], in_=kbs[nb][:], func=ACT.Copy, bias=EPS, scale=1.0)
+            for c in range(2):
+                cols = slice(2 * P * c, 2 * P * (c + 1))
+                if c < GRAM[nb] // 2:
+                    nc.scalar.activation(out=ksb[:, cols], in_=kbs[nb][:, cols], func=ACT.Copy, bias=EPS, scale=1.0)
+                else:
+                    nc.scalar.activation(
+                        out=ksb[:, cols].rearrange("p (w e) -> p w e", e=2),
+                        in_=kbs[nb][:, cols].rearrange("p (e w) -> p w e", e=2),
+                        func=ACT.Copy, bias=EPS, scale=1.0,
+                    )
             ksbs[nb] = ksb
 
         def cb_bcast(nb):
@@ -426,8 +436,6 @@ def tile_yatnmn_kernel(tc, x, kernel, bias, alpha, out_0, out_1):
             step(1, True)
             step(2, True)
             act()
-            fill()
-            diag(1)
 
             for j in range(1, NB):
                 for q in range(NG * (j + 2), NG * (j + 3)):
@@ -442,20 +450,16 @@ def tile_yatnmn_kernel(tc, x, kernel, bias, alpha, out_0, out_1):
                     cb_bcast(j)
                     cb_evac(j)
                 quant(NG * j + 2)
-                if j > 1:
-                    ksq_reduce(j)
-                    ksq_bcast(j)
+                if j == 1:
+                    diag(1)
+                ksq_reduce(j)
+                ksq_bcast(j)
                 quant(NG * j + 3)
+                ksq_evac(j)
                 quant(NG * j)
                 if j + 1 < NB:
                     inter_s(NG * (j + 1))
-                if j > 1:
-                    ksq_evac(j)
                 quant(NG * j + 1)
-                if j == 1:
-                    ksq_reduce(j)
-                    ksq_bcast(j)
-                    ksq_evac(j)
                 if j + 1 < NB:
                     for g in (1, 2, 3):
                         inter_g(NG * (j + 1) + g)
@@ -463,6 +467,8 @@ def tile_yatnmn_kernel(tc, x, kernel, bias, alpha, out_0, out_1):
                 issue_mx(4 * j)
                 fill()
                 issue_mx(4 * j + 1)
+                if j == 1:
+                    fill()
                 if j + 1 < NB:
                     gram(j + 1, (0,))
                 for t in range(4 * j - 1, 4 * j + 3):

@@ -152,7 +152,9 @@ def tile_yatnmn_kernel(tc, x, kernel, bias, alpha, out_0, out_1):
 
         def inter_v(q):
             new_grp(q)
-            nc.vector.tensor_copy(out=grp[q][:], in_=raw[q][:].rearrange("p j w -> p w j"))
+            nc.vector.tensor_copy(
+                out=grp[q][:].rearrange("p (c i) j -> p c j i", i=4), in_=raw[q][:].rearrange("p j (c i) -> p c j i", i=4)
+            )
 
         def inter_g(q):
             new_grp(q)
@@ -177,7 +179,8 @@ def tile_yatnmn_kernel(tc, x, kernel, bias, alpha, out_0, out_1):
 
         def inter_v_rest(q):
             nc.vector.tensor_copy(
-                out=grp[q][:, CS + CG:NW, :], in_=raw[q][:, :, CS + CG:NW].rearrange("p j w -> p w j")
+                out=grp[q][:, CS + CG:NW, :].rearrange("p (c i) j -> p c j i", i=4),
+                in_=raw[q][:, :, CS + CG:NW].rearrange("p j (c i) -> p c j i", i=4),
             )
 
         def quant(q):

@@ -159,7 +159,8 @@ def tile_yatnmn_kernel(tc, x, kernel, bias, alpha, out_0, out_1):
         def inter_g(q):
             new_grp(q)
             nc.gpsimd.tensor_scalar(
-                out=grp[q][:], in0=raw[q][:].rearrange("p j w -> p w j"), scalar1=1.0, scalar2=0.0,
+                out=grp[q][:].rearrange("p (c i) j -> p c j i", i=4),
+                in0=raw[q][:].rearrange("p j (c i) -> p c j i", i=4), scalar1=1.0, scalar2=0.0,
                 op0=ALU.mult, op1=ALU.add,
             )
 
@@ -173,7 +174,8 @@ def tile_yatnmn_kernel(tc, x, kernel, bias, alpha, out_0, out_1):
 
         def inter_g_rest(q):
             nc.gpsimd.tensor_scalar(
-                out=grp[q][:, CS:CS + CG, :], in0=raw[q][:, :, CS:CS + CG].rearrange("p j w -> p w j"),
+                out=grp[q][:, CS:CS + CG, :].rearrange("p (c i) j -> p c j i", i=4),
+                in0=raw[q][:, :, CS:CS + CG].rearrange("p j (c i) -> p c j i", i=4),
                 scalar1=1.0, scalar2=0.0, op0=ALU.mult, op1=ALU.add,
             )
 

@@ -31,8 +31,8 @@ GRP_TAG = ("g0", "gA", "gB", "gC")
 GRAM = (2, 2, 2, 0, 2, 2, 2, 0)
 GADD_FROM = 24
 GADD_TO = 31
-CS = 192
-CG = 192
+CS = 128
+CG = 384
 
 FLOPS = 2 * TOK * D * O
 
@@ -448,7 +448,6 @@ def tile_yatnmn_kernel(tc, x, kernel, bias, alpha, out_0, out_1):
                         load_raw(q)
                 if j > 1:
                     cb_bcast(j - 1)
-                    inter_v_rest(NG * j)
                 act()
                 if NM * (j - 1) >= GADD_FROM:
                     cb_evac(j - 1)

@@ -166,11 +166,16 @@ def tile_yatnmn_kernel(tc, x, kernel, bias, alpha, out_0, out_1):
 
         def inter_s(q):
             new_grp(q)
-            nc.scalar.copy(out=grp[q][:, 0:CS, :], in_=raw[q][:, :, 0:CS].rearrange("p j w -> p w j"))
+            nc.scalar.copy(
+                out=grp[q][:, 0:CS, :].rearrange("p (c i) j -> p c j i", i=4),
+                in_=raw[q][:, :, 0:CS].rearrange("p j (c i) -> p c j i", i=4),
+            )
 
         def inter_s_whole(q):
             new_grp(q)
-            nc.scalar.copy(out=grp[q][:], in_=raw[q][:].rearrange("p j w -> p w j"))
+            nc.scalar.copy(
+                out=grp[q][:].rearrange("p (c i) j -> p c j i", i=4), in_=raw[q][:].rearrange("p j (c i) -> p c j i", i=4)
+            )
 
         def inter_g_rest(q):
             nc.gpsimd.tensor_scalar(

@@ -135,6 +135,14 @@ def tile_yatnmn_kernel(tc, x, kernel, bias, alpha, out_0, out_1):
                     in_=xts[(m, gp)][:].rearrange("p g u r -> p g r u"),
                 )
 
+        def x_evac_half(m, gp):
+            if gp == 0:
+                xgs[m] = grpp.tile([P, NG, P, 4], BF16, name="xg%d" % m, tag="xg", bufs=2, align_bytes=64)
+            nc.vector.tensor_copy(
+                out=xgs[m][:, 2 * gp:2 * gp + 2, :, :].bitcast(F32),
+                in_=xts[(m, gp)][:].rearrange("p g u r -> p g r u"),
+            )
+
         def x_square(m):
             junk = smlp.tile([P, D], BF16, name="junkx%d" % m, tag="junk")
             nc.scalar.activation(out=junk[:], in_=xsb[m][:], func=ACT.Square, accum_out=xsq[:, m:m + 1])
@@ -248,6 +256,24 @@ def tile_yatnmn_kernel(tc, x, kernel, bias, alpha, out_0, out_1):
                 nc.vector.scalar_tensor_tensor(
                     out=junkf[:], in0=gks[nb][:, ob, :], scalar=1.0, in1=ident_f[:], op0=ALU.mult,
                     op1=ALU.mult, accum_out=ksq_cols[:, col:col + 1],
+                )
+
+        gh = {}
+
+        def gram_head(g):
+            for ob in range(2):
+                for j in range(4):
+                    kk = raw[g][:, j, P * ob:P * (ob + 1)]
+                    nc.tensor.matmul(
+                        out=gh[ob][:], lhsT=kk, rhs=kk, start=(g == 0 and j == 0), stop=(g == NG - 1 and j == 3)
+                    )
+
+        def diag_head():
+            for ob in range(2):
+                junkf = tmpp.tile([P, P], F32, name="junkh%d" % ob, tag="jf", bufs=2)
+                nc.vector.scalar_tensor_tensor(
+                    out=junkf[:], in0=gh[ob][:], scalar=1.0, in1=ident_f[:], op0=ALU.mult,
+                    op1=ALU.mult, accum_out=ksq_cols[:, 4 * ob:4 * ob + 1],
                 )
 
         def ksq_reduce(nb):
@@ -375,11 +401,11 @@ def tile_yatnmn_kernel(tc, x, kernel, bias, alpha, out_0, out_1):
         nc.scalar.dma_start(out=alpha_t[:], in_=alpha.partition_broadcast(P))
         nc.vector.memset(bias_rows[:], 0.0)
         nc.scalar.dma_start(out=bias_rows[0:O // P, :], in_=bias.rearrange("(r c) -> r c", c=P))
-        for m in range(NM):
-            load_x(m)
-        for q in range(8):
+        for i in range(4):
+            load_raw(i)
+            load_x(i)
+        for q in range(4, 8):
             load_raw(q)
-
         make_identity(nc, ident_f[:])
         make_identity(nc, ident_bf[:])
         nc.vector.memset(zero[:], 0.0)
@@ -389,64 +415,87 @@ def tile_yatnmn_kernel(tc, x, kernel, bias, alpha, out_0, out_1):
         nc.scalar.activation(out=dummy[:], in_=c_t[:], func=ACT.Abs_reciprocal_sqrt)
 
         with tc.manual_schedule():
-            for m in range(NM):
-                x_trans(m)
-                x_square(m)
-                x_evac(m)
-                if m > 0:
-                    x_quant(m - 1)
+            bias_t = psc.tile([P, P], BF16, name="bias_t", tag="cb")
+            nc.tensor.transpose(out=bias_t[:], in_=bias_rows[:], identity=ident_bf[:])
+            nc.vector.tensor_scalar(out=cbcol[:], in0=bias_t[:, 0:O // P], scalar1=c_t[:, 0:1], scalar2=None, op0=ALU.mult)
+            gh[0] = psm.tile([P, P], F32, name="gh0", tag="misc")
+            gh[1] = psc.tile([P, P], F32, name="gh1", tag="cb")
             inter_v(0)
-            x_quant(3)
             fill()
-            fill()
+            gram_head(0)
+            x_trans(0)
+            x_square(0)
+            x_evac_half(0, 0)
             inter_v(1)
-            quant(0)
             act()
             fill()
+            gram_head(1)
+            x_evac_half(0, 1)
+            quant(0)
+            x_trans(1)
+            x_square(1)
+            x_quant(0)
+            x_evac_half(1, 0)
             inter_v(2)
             act()
             fill()
+            gram_head(2)
+            x_evac_half(1, 1)
             quant(1)
+            x_trans(2)
+            x_square(2)
+            x_quant(1)
+            x_evac_half(2, 0)
+            x_evac_half(2, 1)
             inter_v(3)
-            gram(0, (0, 1))
-            bias_t = psc.tile([P, P], BF16, name="bias_t", tag="cb")
-            nc.tensor.transpose(out=bias_t[:], in_=bias_rows[:], identity=ident_bf[:])
-            act()
             act()
             fill()
-            fill()
+            gram_head(3)
             quant(2)
-            inter_s_whole(NG)
+            x_trans(3)
             act()
-            diag(0)
-            nc.vector.tensor_scalar(
-                out=cbcol[:], in0=bias_t[:, 0:O // P], scalar1=c_t[:, 0:1], scalar2=None, op0=ALU.mult
-            )
             quant(3)
             issue_mx(0)
+            x_square(3)
+            diag_head()
             ksq_reduce(0)
-            act()
-            ksq_bcast(0)
             fill()
+            ksq_bcast(0)
+            x_quant(2)
             ksq_evac(0)
             issue_mx(1)
+            x_evac_half(3, 0)
+            x_evac_half(3, 1)
+            x_quant(3)
             fill()
-            for q in range(8, 12):
-                load_raw(q)
+            issue_mx(2)
+            cb_bcast(0)
+            load_raw(8)
+            load_raw(9)
+            load_raw(10)
+            load_raw(11)
+            inter_g(NG + 3)
+            issue_mx(3)
+            dprime(0)
+            act()
+            fill()
+            dprime(1)
+            act()
+            gram(1, (0, 1))
+            fill()
+            dprime(2)
+            umul(0)
+            act()
+            fill()
+            umul(1)
+            inter_v(NG)
+            act()
+            fill()
             inter_v(NG + 1)
             act()
-            cb_bcast(0)
-            issue_mx(2)
             fill()
             inter_v(NG + 2)
-            gram(1, (0, 1))
-            issue_mx(3)
-            inter_v(NG + 3)
-            step(0, False)
-            step(1, True)
-            step(2, True)
             act()
-
             for j in range(1, NB):
                 for q in range(NG * (j + 2), NG * (j + 3)):
                     if q < NSTEP:

@@ -415,9 +415,6 @@ def tile_yatnmn_kernel(tc, x, kernel, bias, alpha, out_0, out_1):
         nc.scalar.activation(out=dummy[:], in_=c_t[:], func=ACT.Abs_reciprocal_sqrt)
 
         with tc.manual_schedule():
-            bias_t = psc.tile([P, P], BF16, name="bias_t", tag="cb")
-            nc.tensor.transpose(out=bias_t[:], in_=bias_rows[:], identity=ident_bf[:])
-            nc.vector.tensor_scalar(out=cbcol[:], in0=bias_t[:, 0:O // P], scalar1=c_t[:, 0:1], scalar2=None, op0=ALU.mult)
             gh[0] = psm.tile([P, P], F32, name="gh0", tag="misc")
             gh[1] = psc.tile([P, P], F32, name="gh1", tag="cb")
             inter_v(0)
@@ -469,13 +466,14 @@ def tile_yatnmn_kernel(tc, x, kernel, bias, alpha, out_0, out_1):
             x_quant(3)
             fill()
             issue_mx(2)
-            cb_bcast(0)
             load_raw(8)
             load_raw(9)
             load_raw(10)
             load_raw(11)
             inter_g(NG + 3)
             issue_mx(3)
+            bias_t = psc.tile([P, P], BF16, name="bias_t", tag="cb")
+            nc.tensor.transpose(out=bias_t[:], in_=bias_rows[:], identity=ident_bf[:])
             dprime(0)
             act()
             fill()
@@ -483,11 +481,13 @@ def tile_yatnmn_kernel(tc, x, kernel, bias, alpha, out_0, out_1):
             act()
             gram(1, (0, 1))
             fill()
-            dprime(2)
             umul(0)
+            dprime(2)
             act()
             fill()
             umul(1)
+            nc.vector.tensor_scalar(out=cbcol[:], in0=bias_t[:, 0:O // P], scalar1=c_t[:, 0:1], scalar2=None, op0=ALU.mult)
+            cb_bcast(0)
             inter_v(NG)
             act()
             fill()

@@ -73,8 +73,8 @@ def tile_yatnmn_kernel(tc, x, kernel, bias, alpha, out_0, out_1):
         amax_cols = keep.tile([P, NSTEP], F32, name="amax_cols")
         pmax = keep.tile([P, 1], F32, name="pmax")
         amax = keep.tile([P, 1], F32, name="amax")
-        ramax = keep.tile([P, 1], F32, name="ramax")
         fac = keep.tile([P, 1], F32, name="fac")
+        gate = keep.tile([P, 1], F32, name="gate")
 
         raw = {}
         grp = {}
@@ -161,7 +161,7 @@ def tile_yatnmn_kernel(tc, x, kernel, bias, alpha, out_0, out_1):
         def inter_v(q):
             new_grp(q)
             nc.vector.tensor_copy(
-                out=grp[q][:].rearrange("p (c i) j -> p c j i", i=4), in_=raw[q][:].rearrange("p j (c i) -> p c j i", i=4)
+                out=grp[q][:].rearrange("p (c i) j -> p c j i", i=8), in_=raw[q][:].rearrange("p j (c i) -> p c j i", i=8)
             )
 
         def inter_g(q):
@@ -169,6 +169,14 @@ def tile_yatnmn_kernel(tc, x, kernel, bias, alpha, out_0, out_1):
             nc.gpsimd.tensor_scalar(
                 out=grp[q][:].rearrange("p (c i) j -> p c j i", i=4),
                 in0=raw[q][:].rearrange("p j (c i) -> p c j i", i=4), scalar1=1.0, scalar2=0.0,
+                op0=ALU.mult, op1=ALU.add,
+            )
+
+        def inter_g_gated(q):
+            new_grp(q)
+            nc.gpsimd.tensor_scalar(
+                out=grp[q][:].rearrange("p (c i) j -> p c j i", i=4),
+                in0=raw[q][:].rearrange("p j (c i) -> p c j i", i=4), scalar1=1.0, scalar2=gate[:, 0:1],
                 op0=ALU.mult, op1=ALU.add,
             )
 
@@ -470,7 +478,8 @@ def tile_yatnmn_kernel(tc, x, kernel, bias, alpha, out_0, out_1):
             load_raw(9)
             load_raw(10)
             load_raw(11)
-            inter_g(NG + 3)
+            nc.vector.memset(gate[:], 0.0)
+            inter_g_gated(NG + 3)
             issue_mx(3)
             bias_t = psc.tile([P, P], BF16, name="bias_t", tag="cb")
             nc.tensor.transpose(out=bias_t[:], in_=bias_rows[:], identity=ident_bf[:])
@@ -551,9 +560,11 @@ def tile_yatnmn_kernel(tc, x, kernel, bias, alpha, out_0, out_1):
         nc.vector.tensor_reduce(out=pmax[:], in_=amax_cols[:], axis=AX.X, op=ALU.max)
         pt = psm.tile([P, P], F32, name="pt", tag="misc")
         nc.tensor.transpose(out=pt[:], in_=pmax[:, 0:1].to_broadcast([P, P]), identity=ident_f[:])
-        nc.vector.tensor_reduce(out=amax[:], in_=pt[:], axis=AX.X, op=ALU.max)
-        nc.vector.reciprocal(out=ramax[:], in_=amax[:])
-        nc.vector.tensor_scalar(out=fac[:], in0=ramax[:], scalar1=448.0, scalar2=None, op0=ALU.mult)
+        ptj = tmpp.tile([P, P], F32, name="ptj", tag="jf", bufs=2)
+        nc.vector.tensor_scalar(
+            out=ptj[:], in0=pt[:], scalar1=1.0 / 448.0, scalar2=None, op0=ALU.mult, op1=ALU.max, accum_out=amax[:]
+        )
+        nc.vector.reciprocal(out=fac[:], in_=amax[:])
         for m in range(NM):
             for h in range(2):
                 c0 = 2048 * h

import math
from contextlib import ExitStack

import concourse.mybir as mybir
from concourse.masks import make_identity

F32 = mybir.dt.float32
BF16 = mybir.dt.bfloat16
U32 = mybir.dt.uint32
U8 = mybir.dt.uint8
FP8X4 = mybir.dt.float8_e4m3fn_x4
FP8 = mybir.dt.float8_e4m3fn
ALU = mybir.AluOpType
ACT = mybir.ActivationFunctionType
AX = mybir.AxisListType

P = 128
TOK = 512
D = 2048
O = 4096
NB = 8
NW = 512
NG = 4
NM = 4
NSTEP = NB * NM
EPS = 1.0 / 137.0
LOG_RATIO = math.log(math.sqrt(4096.0) / math.log(1.0 + 4096.0))
CV = 1408
PASS_ORDER = (2, 3, 0, 1)
GRP_TAG = ("g0", "gA", "gB", "gC")
GRAM = (2, 2, 2, 0, 2, 2, 2, 0)
GADD_FROM = 24
GADD_TO = 31
CS = 128
CG = 384

FLOPS = 2 * TOK * D * O


def tile_yatnmn_kernel(tc, x, kernel, bias, alpha, out_0, out_1):
    nc = tc.nc
    xf = x.flatten_outer_dims()
    o0 = out_0.flatten_outer_dims()
    o1 = out_1.flatten_outer_dims()

    with ExitStack() as ctx:
        keep = ctx.enter_context(tc.tile_pool(name="keep", bufs=1))
        rawp = ctx.enter_context(tc.tile_pool(name="rawp", bufs=12))
        grpp = ctx.enter_context(tc.tile_pool(name="grpp", bufs=1))
        codp = ctx.enter_context(tc.tile_pool(name="codp", bufs=8))
        tmpp = ctx.enter_context(tc.tile_pool(name="tmpp", bufs=4))
        smlp = ctx.enter_context(tc.tile_pool(name="smlp", bufs=2))
        psy = ctx.enter_context(tc.psum_pool(name="psy", bufs=4))
        psk = ctx.enter_context(tc.psum_pool(name="psk", bufs=2))
        psc = ctx.enter_context(tc.psum_pool(name="psc", bufs=1))
        psm = ctx.enter_context(tc.psum_pool(name="psm", bufs=1))

        out_sb = keep.tile([P, NM, O], F32, name="out_sb")
        q8 = keep.tile([P, NM, O], FP8, name="q8")
        xc = keep.tile([P, NM, NG * P], U32, name="xc", align_bytes=64)
        xs = keep.tile([P, NM, NG * P], U8, name="xs", align_bytes=64)
        ident_bf = keep.tile([P, P], BF16, name="ident_bf")
        ident_f = keep.tile([P, P], F32, name="ident_f")
        bias_rows = keep.tile([P, P], BF16, name="bias_rows")
        cbcol = keep.tile([P, O // P], F32, name="cbcol")
        alpha_t = keep.tile([P, 1], BF16, name="alpha_t")
        c_t = keep.tile([P, 1], F32, name="c_t")
        sc_t = keep.tile([P, 1], F32, name="sc_t")
        dummy = keep.tile([P, 1], F32, name="dummy")
        zero = keep.tile([P, 1], F32, name="zero")
        xsq = keep.tile([P, NM], F32, name="xsq")
        ksq_cols = keep.tile([P, 16 * NB], F32, name="ksq_cols")
        amax_cols = keep.tile([P, NSTEP], F32, name="amax_cols")
        pmax = keep.tile([P, 1], F32, name="pmax")
        amax = keep.tile([P, 1], F32, name="amax")
        fac = keep.tile([P, 1], F32, name="fac")
        gate = keep.tile([P, 1], F32, name="gate")

        raw = {}
        grp = {}
        kc = {}
        ks = {}
        kts = {}
        gks = {}
        k4s = {}
        kbs = {}
        ksbs = {}
        cbs = {}
        cbsb = {}
        ys = {}
        t1s = {}
        t2s = {}
        xsb = {}
        xts = {}
        xgs = {}

        stream = []
        for nb in range(NB):
            for g in range(NG):
                for c in range(GRAM[nb] // 2, 2):
                    stream.append((nb, c, g))
        state = {"fill": 0, "act": 0, "mx": 0, "kq": -1, "xq": -1}

        def load_raw(q):
            nb, g = divmod(q, NG)
            t = rawp.tile([P, 4, NW], BF16, name="raw%d" % q, tag="raw")
            nc.sync.dma_start(
                out=t[:],
                in_=kernel[512 * g:512 * (g + 1), NW * nb:NW * (nb + 1)].rearrange("(p j) w -> p j w", j=4),
            )
            raw[q] = t

        def load_x(m):
            t = rawp.tile([P, D], BF16, name="xsb%d" % m, tag="raw")
            nc.sync.dma_start(out=t[:], in_=xf[P * m:P * (m + 1), :])
            xsb[m] = t

        def x_trans(m):
            words = xsb[m][:].bitcast(F32)
            for gp in range(2):
                xt = psy.tile([P, 2, 2, P], F32, name="xt%d_%d" % (m, gp), tag="y")
                for gi in range(2):
                    g = 2 * gp + gi
                    for u in range(2):
                        nc.tensor.transpose(
                            out=xt[:, gi, u, :], in_=words[:, 256 * g + u:256 * (g + 1):2], identity=ident_f[:]
                        )
                xts[(m, gp)] = xt

        def x_evac(m):
            xgs[m] = grpp.tile([P, NG, P, 4], BF16, name="xg%d" % m, tag="xg", bufs=2, align_bytes=64)
            for gp in range(2):
                nc.vector.tensor_copy(
                    out=xgs[m][:, 2 * gp:2 * gp + 2, :, :].bitcast(F32),
                    in_=xts[(m, gp)][:].rearrange("p g u r -> p g r u"),
                )

        def x_evac_half(m, gp):
            if gp == 0:
                xgs[m] = grpp.tile([P, NG, P, 4], BF16, name="xg%d" % m, tag="xg", bufs=2, align_bytes=64)
            nc.vector.tensor_copy(
                out=xgs[m][:, 2 * gp:2 * gp + 2, :, :].bitcast(F32),
                in_=xts[(m, gp)][:].rearrange("p g u r -> p g r u"),
            )

        def x_square(m):
            junk = smlp.tile([P, D], BF16, name="junkx%d" % m, tag="junk")
            nc.scalar.activation(out=junk[:], in_=xsb[m][:], func=ACT.Square, accum_out=xsq[:, m:m + 1])

        def x_quant(m):
            nc.vector.quantize_mx(
                out=xc[:, m, :].bitcast(FP8X4),
                scales=xs[:, m, :],
                in_=xgs[m][:].rearrange("p g r j -> p (g r j)"),
            )
            state["xq"] = m

        def new_grp(q):
            grp[q] = grpp.tile([P, NW, 4], BF16, name="grp%d" % q, tag=GRP_TAG[q % NG], bufs=1, align_bytes=64)

        def inter_v(q):
            new_grp(q)
            nc.vector.tensor_copy(
                out=grp[q][:].rearrange("p (c i) j -> p c j i", i=8), in_=raw[q][:].rearrange("p j (c i) -> p c j i", i=8)
            )

        def inter_g(q):
            new_grp(q)
            nc.gpsimd.tensor_scalar(
                out=grp[q][:].rearrange("p (c i) j -> p c j i", i=4),
                in0=raw[q][:].rearrange("p j (c i) -> p c j i", i=4), scalar1=1.0, scalar2=0.0,
                op0=ALU.mult, op1=ALU.add,
            )

        def inter_g_gated(q):
            new_grp(q)
            nc.gpsimd.tensor_scalar(
                out=grp[q][:].rearrange("p (c i) j -> p c j i", i=4),
                in0=raw[q][:].rearrange("p j (c i) -> p c j i", i=4), scalar1=1.0, scalar2=gate[:, 0:1],
                op0=ALU.mult, op1=ALU.add,
            )

        def inter_s(q):
            new_grp(q)
            nc.scalar.copy(
                out=grp[q][:, 0:CS, :].rearrange("p (c i) j -> p c j i", i=4),
                in_=raw[q][:, :, 0:CS].rearrange("p j (c i) -> p c j i", i=4),
            )

        def inter_s_whole(q):
            new_grp(q)
            nc.scalar.copy(
                out=grp[q][:].rearrange("p (c i) j -> p c j i", i=4), in_=raw[q][:].rearrange("p j (c i) -> p c j i", i=4)
            )

        def inter_g_rest(q):
            nc.gpsimd.tensor_scalar(
                out=grp[q][:, CS:CS + CG, :].rearrange("p (c i) j -> p c j i", i=4),
                in0=raw[q][:, :, CS:CS + CG].rearrange("p j (c i) -> p c j i", i=4),
                scalar1=1.0, scalar2=0.0, op0=ALU.mult, op1=ALU.add,
            )

        def inter_v_rest(q):
            nc.vector.tensor_copy(
                out=grp[q][:, CS + CG:NW, :].rearrange("p (c i) j -> p c j i", i=4),
                in_=raw[q][:, :, CS + CG:NW].rearrange("p j (c i) -> p c j i", i=4),
            )

        def quant(q):
            c = codp.tile([P, NW], U32, name="kc%d" % q, tag="kc", align_bytes=64)
            s = codp.tile([P, NW], U8, name="ks%d" % q, tag="ks", align_bytes=64)
            nc.vector.quantize_mx(out=c[:].bitcast(FP8X4), scales=s[:], in_=grp[q][:].rearrange("p w j -> p (w j)"))
            kc[q] = c
            ks[q] = s
            if q % NG == PASS_ORDER[3]:
                state["kq"] = q // NG

        def fill():
            t = state["fill"]
            if t >= len(stream):
                return
            state["fill"] = t + 1
            nb, c, g = stream[t]
            kt = psk.tile([P, 4, P], F32, name="kt%d" % t, tag="kT")
            words = raw[NG * nb + g][:].bitcast(F32)
            for j in range(4):
                nc.tensor.transpose(out=kt[:, j, :], in_=words[:, j, P * c:P * (c + 1)], identity=ident_f[:])
            kts[t] = kt

        def act():
            t = state["act"]
            if t >= len(stream):
                return
            state["act"] = t + 1
            nb, c, g = stream[t]
            halves = kts[t][:].rearrange("p j q -> p (j q)").bitcast(BF16).rearrange("p (n e) -> p n e", e=2)
            for e in range(2):
                col = 16 * nb + 8 * c + 4 * e + g
                junk = smlp.tile([P, 4 * P], BF16, name="junk%d_%d" % (t, e), tag="junk")
                nc.scalar.activation(
                    out=junk[:], in_=halves[:, :, e], func=ACT.Square, accum_out=ksq_cols[:, col:col + 1]
                )

        def gram(nb, tiles):
            if GRAM[nb] == 0:
                return
            if 0 in tiles:
                gks[nb] = psm.tile([P, GRAM[nb], P], F32, name="gk%d" % nb, tag="misc")
            gk = gks[nb]
            for ob in tiles:
                if ob >= GRAM[nb]:
                    continue
                for g in range(NG):
                    for j in range(4):
                        kk = raw[NG * nb + g][:, j, P * ob:P * (ob + 1)]
                        nc.tensor.matmul(
                            out=gk[:, ob, :], lhsT=kk, rhs=kk, start=(g == 0 and j == 0), stop=(g == NG - 1 and j == 3)
                        )

        def diag(nb):
            for ob in range(GRAM[nb]):
                junkf = tmpp.tile([P, P], F32, name="junkg%d_%d" % (nb, ob), tag="jf", bufs=2)
                col = 16 * nb + 4 * ob
                nc.vector.scalar_tensor_tensor(
                    out=junkf[:], in0=gks[nb][:, ob, :], scalar=1.0, in1=ident_f[:], op0=ALU.mult,
                    op1=ALU.mult, accum_out=ksq_cols[:, col:col + 1],
                )

        gh = {}

        def gram_head(g):
            for ob in range(2):
                for j in range(4):
                    kk = raw[g][:, j, P * ob:P * (ob + 1)]
                    nc.tensor.matmul(
                        out=gh[ob][:], lhsT=kk, rhs=kk, start=(g == 0 and j == 0), stop=(g == NG - 1 and j == 3)
                    )

        def diag_head():
            for ob in range(2):
                junkf = tmpp.tile([P, P], F32, name="junkh%d" % ob, tag="jf", bufs=2)
                nc.vector.scalar_tensor_tensor(
                    out=junkf[:], in0=gh[ob][:], scalar=1.0, in1=ident_f[:], op0=ALU.mult,
                    op1=ALU.mult, accum_out=ksq_cols[:, 4 * ob:4 * ob + 1],
                )

        def ksq_reduce(nb):
            k4 = smlp.tile([P, 4], F32, name="k4_%d" % nb, tag="k4")
            nc.vector.tensor_reduce(
                out=k4[:],
                in_=ksq_cols[:, 16 * nb:16 * (nb + 1)].rearrange("p (o h) -> p o h", h=4),
                axis=AX.X,
                op=ALU.add,
            )
            k4s[nb] = k4

        def ksq_bcast(nb):
            kb = psm.tile([P, NW], F32, name="kb%d" % nb, tag="misc")
            for ob in range(4):
                nc.tensor.transpose(
                    out=kb[:, P * ob:P * (ob + 1)],
                    in_=k4s[nb][:, ob:ob + 1].to_broadcast([P, P]),
                    identity=ident_f[:],
                )
            kbs[nb] = kb

        def ksq_evac(nb):
            ksb = smlp.tile([P, NW], F32, name="ksb%d" % nb, tag="ksb")
            for c in range(2):
                cols = slice(2 * P * c, 2 * P * (c + 1))
                if c < GRAM[nb] // 2:
                    nc.scalar.activation(out=ksb[:, cols], in_=kbs[nb][:, cols], func=ACT.Copy, bias=EPS, scale=1.0)
                else:
                    nc.scalar.activation(
                        out=ksb[:, cols].rearrange("p (w e) -> p w e", e=2),
                        in_=kbs[nb][:, cols].rearrange("p (e w) -> p w e", e=2),
                        func=ACT.Copy, bias=EPS, scale=1.0,
                    )
            ksbs[nb] = ksb

        def cb_bcast(nb):
            cb = psc.tile([P, NW], F32, name="cb%d" % nb, tag="cb")
            for ob in range(4):
                i = 4 * nb + ob
                nc.tensor.transpose(
                    out=cb[:, P * ob:P * (ob + 1)],
                    in_=cbcol[:, i:i + 1].to_broadcast([P, P]),
                    identity=ident_f[:],
                )
            cbs[nb] = cb

        def mx(s):
            nb, m = divmod(s, NM)
            ys[s] = psy.tile([P, NW], F32, name="y%d" % s, tag="y")
            for g in PASS_ORDER:
                nc.tensor.matmul_mx(
                    out=ys[s][:],
                    lhsT=xc[:, m, P * g:P * (g + 1)].bitcast(FP8X4),
                    lhsT_scale=xs[:, m, P * g:P * (g + 1)],
                    rhs=kc[NG * nb + g][:].bitcast(FP8X4),
                    rhs_scale=ks[NG * nb + g][:],
                    start=(g == PASS_ORDER[0]),
                    stop=(g == PASS_ORDER[3]),
                )

        def dprime(s):
            nb, m = divmod(s, NM)
            t1 = tmpp.tile([P, NW], F32, name="t1_%d" % s, tag="t1")
            nc.vector.scalar_tensor_tensor(
                out=t1[:], in0=ys[s][:], scalar=-2.0, in1=ksbs[nb][:], op0=ALU.mult, op1=ALU.add
            )
            t1s[s] = t1
            nc.scalar.activation(
                out=t1[:], in_=t1[:], func=ACT.Abs_reciprocal_sqrt, bias=xsq[:, m:m + 1], scale=1.0
            )

        def umul(s):
            t2 = tmpp.tile([P, NW], F32, name="t2_%d" % s, tag="t2")
            nc.vector.tensor_tensor(out=t2[:], in0=ys[s][:], in1=t1s[s][:], op=ALU.mult)
            t2s[s] = t2
            nc.scalar.activation(out=t2[:], in_=t2[:], func=ACT.Square, scale=sc_t[:, 0:1])

        def cb_evac(nb):
            t = smlp.tile([P, NW], F32, name="cbsb%d" % nb, tag="cbsb")
            nc.scalar.copy(out=t[:], in_=cbs[nb][:])
            cbsb[nb] = t

        def addb(s):
            nb, m = divmod(s, NM)
            cols = slice(NW * nb, NW * (nb + 1))
            if GADD_FROM <= s < GADD_TO:
                nc.gpsimd.tensor_tensor(out=out_sb[:, m, cols], in0=t2s[s][:], in1=cbsb[nb][:], op=ALU.add)
            else:
                nc.vector.tensor_tensor(out=out_sb[:, m, cols], in0=t2s[s][:], in1=cbs[nb][:], op=ALU.add)
            nc.sync.dma_start(out=o0[P * m:P * (m + 1), cols], in_=out_sb[:, m, cols])

        def absmax(s):
            nb, m = divmod(s, NM)
            nc.vector.tensor_reduce(
                out=amax_cols[:, s:s + 1], in_=out_sb[:, m, NW * nb:NW * (nb + 1)],
                axis=AX.X, op=ALU.max, apply_absolute_value=True,
            )

        def ok(s):
            return 0 <= s < NSTEP

        def issue_mx(last):
            while state["mx"] <= min(last, NSTEP - 1):
                s = state["mx"]
                if s // NM > state["kq"] or (s < NM and s > state["xq"]):
                    return
                mx(s)
                state["mx"] = s + 1

        def step(t, with_act):
            issue_mx(t + 2)
            if ok(t):
                dprime(t)
            if with_act:
                act()
                fill()
            if ok(t - 4):
                absmax(t - 4)
            if ok(t - 3):
                addb(t - 3)
            if ok(t - 1):
                umul(t - 1)

        nc.scalar.dma_start(out=alpha_t[:], in_=alpha.partition_broadcast(P))
        nc.vector.memset(bias_rows[:], 0.0)
        nc.scalar.dma_start(out=bias_rows[0:O // P, :], in_=bias.rearrange("(r c) -> r c", c=P))
        for i in range(4):
            load_raw(i)
            load_x(i)
        for q in range(4, 8):
            load_raw(q)
        make_identity(nc, ident_f[:])
        make_identity(nc, ident_bf[:])
        nc.vector.memset(zero[:], 0.0)
        nc.vector.memset(ksq_cols[:], 0.0)
        nc.scalar.activation(out=c_t[:], in_=alpha_t[:], func=ACT.Exp, scale=LOG_RATIO)
        nc.scalar.activation(out=sc_t[:], in_=alpha_t[:], func=ACT.Exp, scale=0.5 * LOG_RATIO)
        nc.scalar.activation(out=dummy[:], in_=c_t[:], func=ACT.Abs_reciprocal_sqrt)

        with tc.manual_schedule():
            gh[0] = psm.tile([P, P], F32, name="gh0", tag="misc")
            gh[1] = psc.tile([P, P], F32, name="gh1", tag="cb")
            inter_v(0)
            fill()
            gram_head(0)
            x_trans(0)
            x_square(0)
            x_evac_half(0, 0)
            inter_v(1)
            act()
            fill()
            gram_head(1)
            x_evac_half(0, 1)
            quant(0)
            x_trans(1)
            x_square(1)
            x_quant(0)
            x_evac_half(1, 0)
            inter_v(2)
            act()
            fill()
            gram_head(2)
            x_evac_half(1, 1)
            quant(1)
            x_trans(2)
            x_square(2)
            x_quant(1)
            x_evac_half(2, 0)
            x_evac_half(2, 1)
            inter_v(3)
            act()
            fill()
            gram_head(3)
            quant(2)
            x_trans(3)
            act()
            quant(3)
            issue_mx(0)
            x_square(3)
            diag_head()
            ksq_reduce(0)
            fill()
            ksq_bcast(0)
            x_quant(2)
            ksq_evac(0)
            issue_mx(1)
            x_evac_half(3, 0)
            x_evac_half(3, 1)
            x_quant(3)
            fill()
            issue_mx(2)
            load_raw(8)
            load_raw(9)
            load_raw(10)
            load_raw(11)
            nc.vector.memset(gate[:], 0.0)
            inter_g_gated(NG + 3)
            issue_mx(3)
            bias_t = psc.tile([P, P], BF16, name="bias_t", tag="cb")
            nc.tensor.transpose(out=bias_t[:], in_=bias_rows[:], identity=ident_bf[:])
            dprime(0)
            act()
            fill()
            dprime(1)
            act()
            gram(1, (0, 1))
            fill()
            umul(0)
            dprime(2)
            act()
            fill()
            umul(1)
            nc.vector.tensor_scalar(out=cbcol[:], in0=bias_t[:, 0:O // P], scalar1=c_t[:, 0:1], scalar2=None, op0=ALU.mult)
            cb_bcast(0)
            inter_v(NG)
            act()
            fill()
            inter_v(NG + 1)
            act()
            fill()
            inter_v(NG + 2)
            act()
            for j in range(1, NB):
                for q in range(NG * (j + 2), NG * (j + 3)):
                    if q < NSTEP:
                        load_raw(q)
                if j > 1:
                    cb_bcast(j - 1)
                act()
                if NM * (j - 1) >= GADD_FROM:
                    cb_evac(j - 1)
                    cb_bcast(j)
                    cb_evac(j)
                quant(NG * j + 2)
                if j == 1:
                    diag(1)
                ksq_reduce(j)
                ksq_bcast(j)
                quant(NG * j + 3)
                ksq_evac(j)
                quant(NG * j)
                if j + 1 < NB:
                    inter_s(NG * (j + 1))
                quant(NG * j + 1)
                if j + 1 < NB:
                    for g in (1, 2, 3):
                        inter_g(NG * (j + 1) + g)
                    inter_g_rest(NG * (j + 1))
                issue_mx(4 * j)
                fill()
                issue_mx(4 * j + 1)
                if j == 1:
                    fill()
                if j + 1 < NB:
                    gram(j + 1, (0,))
                for t in range(4 * j - 1, 4 * j + 3):
                    step(t, True)
                    if t == 4 * j and j + 1 < NB:
                        gram(j + 1, (1,))
                    if t == 4 * j + 2 and j + 1 < NB:
                        diag(j + 1)
            dprime(NSTEP - 1)
            umul(NSTEP - 2)
            absmax(NSTEP - 5)
            addb(NSTEP - 4)
            absmax(NSTEP - 4)
            umul(NSTEP - 1)
            addb(NSTEP - 3)
            absmax(NSTEP - 3)
            addb(NSTEP - 2)
            absmax(NSTEP - 2)
            addb(NSTEP - 1)
            absmax(NSTEP - 1)

        nc.vector.tensor_reduce(out=pmax[:], in_=amax_cols[:], axis=AX.X, op=ALU.max)
        pt = psm.tile([P, P], F32, name="pt", tag="misc")
        nc.tensor.transpose(out=pt[:], in_=pmax[:, 0:1].to_broadcast([P, P]), identity=ident_f[:])
        ptj = tmpp.tile([P, P], F32, name="ptj", tag="jf", bufs=2)
        nc.vector.tensor_scalar(
            out=ptj[:], in0=pt[:], scalar1=1.0 / 448.0, scalar2=None, op0=ALU.mult, op1=ALU.max, accum_out=amax[:]
        )
        nc.vector.reciprocal(out=fac[:], in_=amax[:])
        for m in range(NM):
            for h in range(2):
                c0 = 2048 * h
                nc.vector.tensor_scalar(
                    out=q8[:, m, c0:c0 + CV], in0=out_sb[:, m, c0:c0 + CV], scalar1=fac[:, 0:1], scalar2=None,
                    op0=ALU.mult, saturate=False,
                )
                nc.scalar.activation(
                    out=q8[:, m, c0 + CV:c0 + 2048], in_=out_sb[:, m, c0 + CV:c0 + 2048], func=ACT.Identity,
                    scale=fac[:, 0:1], bias=zero[:, 0:1], saturate=False,
                )
                nc.sync.dma_start(
                    out=o1[P * m:P * (m + 1), c0:c0 + 2048], in_=q8[:, m, c0:c0 + 2048].bitcast(U8)
                )
